import numpy as np
import ml_dtypes


def mxq(x, axis, fmt="e4m3"):
    dtype, down = {"e4m3": (ml_dtypes.float8_e4m3fn, 7), "e5m2": (ml_dtypes.float8_e5m2, 14)}[fmt]
    v = np.moveaxis(np.asarray(x, np.float32).astype(ml_dtypes.bfloat16).astype(np.float64), axis, -1)
    blocks = v.reshape(v.shape[:-1] + (-1, 32))
    amax = np.abs(blocks).max(-1, keepdims=True)
    byte = np.maximum(np.where(amax > 0, np.frexp(amax)[1] - 1 + 127, 0) - down, 1)
    scale = np.exp2(byte - 127.0)
    codes = (blocks / scale).astype(np.float32).astype(dtype).astype(np.float64)
    return np.moveaxis((codes * scale).reshape(v.shape), -1, axis)


BF16 = ml_dtypes.bfloat16


def bf(x):
    return np.asarray(x, np.float32).astype(BF16)


def f64(x):
    return np.asarray(x).astype(np.float64)


N, M, D, R = 8192, 256, 512, 4
LIM = 36.0


def softplus(v):
    return np.where(v > LIM, v, np.log(1.0 + np.exp(np.minimum(v, LIM))))


def setup_inputs():
    P = np.random.standard_normal((R, D))
    X = (0.6 * np.random.standard_normal((N, R)) @ P + 0.3 * np.random.standard_normal((N, D))) / np.sqrt(D)
    Z = (0.6 * np.random.standard_normal((M, R)) @ P + 0.3 * np.random.standard_normal((M, D))) / np.sqrt(D)
    return {"X": bf(X), "Z": bf(Z), "l_raw": bf(np.random.uniform(0.0, 1.0, D)), "sigma_f_raw": bf(1.0 + 0.1 * np.random.standard_normal(1))}


def reference(X, Z, l_raw, sigma_f_raw):
    l = softplus(f64(l_raw))
    sigma_f = softplus(f64(sigma_f_raw))
    inv_length = 1.0 / (l * l)
    w = np.sqrt(inv_length)
    Xs = f64(X) * w
    Zs = f64(Z) * w
    x2 = np.sum(Xs * Xs, axis=1)
    z2 = np.sum(Zs * Zs, axis=1)
    cross = mxq(Xs, 1, "e4m3") @ mxq(Zs, 1, "e4m3").T
    dist = x2[:, None] + z2[None, :] - 2.0 * cross
    return sigma_f * np.exp(-0.5 * dist)

@@ -1,0 +1,221 @@
+from contextlib import ExitStack
+
+import concourse.mybir as mybir
+from concourse.masks import make_identity
+
+F32 = mybir.dt.float32
+BF16 = mybir.dt.bfloat16
+U32 = mybir.dt.uint32
+U8 = mybir.dt.uint8
+FP8X4 = mybir.dt.float8_e4m3fn_x4
+ALU = mybir.AluOpType
+ACT = mybir.ActivationFunctionType
+
+P = 128
+N_ROWS = 8192
+M_COLS = 256
+D = 512
+LIM = 36.0
+TPC = 8
+PPC = TPC // 2
+CHUNK = P * TPC
+NCH = N_ROWS // CHUNK
+NPAIR = NCH * PPC
+FLOPS = 2 * N_ROWS * M_COLS * D
+
+V_MADE = (5, 13, 21, 29)
+LAG_E1 = 4
+LAG_E2 = 5
+LAG_SQ = 2
+
+
+def tile_rbf_kernel_t_kernel(tc, X, Z, l_raw, sigma_f_raw, out):
+    nc = tc.nc
+    with ExitStack() as ctx:
+        const = ctx.enter_context(tc.tile_pool(name="const", bufs=1))
+        xpool = ctx.enter_context(tc.tile_pool(name="xpool", bufs=NCH))
+        gpool = ctx.enter_context(tc.tile_pool(name="gpool", bufs=2))
+        ypool = ctx.enter_context(tc.tile_pool(name="ypool", bufs=5))
+        jpool = ctx.enter_context(tc.tile_pool(name="jpool", bufs=2))
+        tpool = ctx.enter_context(tc.tile_pool(name="tpool", bufs=4))
+        opool = ctx.enter_context(tc.tile_pool(name="opool", bufs=3))
+        psx = ctx.enter_context(tc.psum_pool(name="psx", bufs=4))
+        psc = ctx.enter_context(tc.psum_pool(name="psc", bufs=4))
+        ctx.enter_context(tc.manual_schedule())
+
+        small = const.tile([P, 32], BF16)
+        nc.vector.memset(small[:], 0.0)
+        with nc.allow_non_contiguous_dma(reason="l_raw, two features to a partition"):
+            nc.sync.dma_start(
+                out=small[:, 0:4].rearrange("p (u e) -> p u e", u=2),
+                in_=l_raw.rearrange("(u p e) -> p u e", u=2, e=2),
+            )
+            nc.scalar.dma_start(out=small[:, 16:17], in_=sigma_f_raw.partition_broadcast(P))
+        z_sb = const.tile([P, 2, D], BF16)
+        nc.sync.dma_start(out=z_sb[:], in_=Z.rearrange("(h p) k -> p h k", p=P))
+        xs = []
+        for c in range(NCH):
+            x_sb = xpool.tile([P, TPC, D], BF16, name="x_sb")
+            nc.sync.dma_start(
+                out=x_sb[:],
+                in_=X[c * CHUNK:(c + 1) * CHUNK, :].rearrange("(p t) k -> p t k", t=TPC),
+            )
+            xs.append(x_sb)
+
+        ident = const.tile([P, P], F32)
+        make_identity(nc, ident[:])
+
+        capped = const.tile([P, 32], F32)
+        nc.vector.tensor_scalar_min(out=capped[:], in0=small[:], scalar1=LIM)
+        expv = const.tile([P, 32], F32)
+        nc.scalar.activation(out=expv[:], in_=capped[:], func=ACT.Exp)
+        logv = const.tile([P, 32], F32)
+        nc.scalar.activation(out=logv[:], in_=expv[:], func=ACT.Ln, bias=1.0)
+        splus = const.tile([P, 32], F32)
+        nc.vector.tensor_tensor(out=splus[:], in0=logv[:], in1=small[:], op=ALU.max)
+        w4 = const.tile([P, 4], F32)
+        nc.vector.reciprocal(out=w4[:], in_=splus[:, 0:4])
+        lnsig = const.tile([P, 1], F32)
+        nc.scalar.activation(out=lnsig[:], in_=splus[:, 16:17], func=ACT.Ln)
+
+        w4_b = w4[:].rearrange("p (o u e) -> p o u e", o=1, u=2).to_broadcast([P, 2 * P, 2, 2])
+
+        def transposes(src_pair, bank):
+            for i, src in enumerate(src_pair):
+                words = src.bitcast(F32)
+                for u in range(2):
+                    nc.tensor.transpose(
+                        bank[:, u, i * P:(i + 1) * P], words[:, u * P:(u + 1) * P], ident[:]
+                    )
+
+        def scale_out(bank, grouped):
+            nc.vector.tensor_tensor(
+                out=grouped.rearrange("p c (u e) -> p c u e", u=2),
+                in0=bank[:].bitcast(BF16).rearrange("p u (c e) -> p c u e", e=2),
+                in1=w4_b,
+                op=ALU.mult,
+            )
+
+        def pair_rows(j):
+            c, q = divmod(j, PPC)
+            return xs[c][:, 2 * q:2 * q + 2, :]
+
+        xbanks = {}
+
+        def stage_t(j):
+            bank = psx.tile([P, 2, 2 * P], F32, name="xbank")
+            rows = pair_rows(j)
+            transposes([rows[:, 0, :], rows[:, 1, :]], bank)
+            xbanks[j] = bank
+
+        zbank = psc.tile([P, 2, 2 * P], F32, tag="cr", name="zbank")
+        transposes([z_sb[:, 0, :], z_sb[:, 1, :]], zbank)
+        rep = const.tile([P, 4, P], F32)
+        nc.vector.tensor_copy(out=rep[:], in_=w4[:].unsqueeze(2).to_broadcast([P, 4, P]))
+        wbank = psc.tile([P, 4, P], F32, tag="cr", name="wbank")
+        for t in range(4):
+            nc.tensor.transpose(wbank[:, t, :], rep[:, t, :], ident[:])
+        for j in range(4):
+            stage_t(j)
+        zgrp = const.tile([P, 2 * P, 4], BF16, align_bytes=64)
+        scale_out(zbank, zgrp[:])
+        w_b = const.tile([P, D], F32)
+        nc.vector.tensor_copy(
+            out=w_b[:].rearrange("m (u p e) -> m u p e", u=2, e=2),
+            in_=wbank[:].rearrange("m (u e) p -> m u p e", u=2),
+        )
+        w_b2 = w_b[:].unsqueeze(1).to_broadcast([P, 2, D])
+        zc = const.tile([P, 2 * P], U32, align_bytes=64)
+        zsc = const.tile([P, 2 * P], U8, align_bytes=64)
+        nc.vector.quantize_mx(
+            out=zc[:].bitcast(FP8X4), scales=zsc[:], in_=zgrp[:].rearrange("p c t -> p (c t)")
+        )
+
+        z2 = const.tile([P, 2], F32)
+        zrep = const.tile([P, 2, P], F32)
+        nz2b = const.tile([P, M_COLS], F32)
+        nz2b2 = nz2b[:].unsqueeze(1).to_broadcast([P, 2, M_COLS])
+        x2 = const.tile([P, 2 * NPAIR], F32)
+        nx2 = const.tile([P, 2 * NPAIR], F32)
+
+        def square_sum(y32, i, acc):
+            junk = jpool.tile([P, D], BF16, name="junk")
+            nc.scalar.activation(out=junk[:], in_=y32[:, i, :], func=ACT.Square, accum_out=acc)
+
+        ys = {}
+        grps = {}
+        quant = {}
+        crs = {}
+        tmps = {}
+        outs = {}
+
+        for j in range(NPAIR + LAG_E2 + 1):
+            g, q = divmod(j, PPC)
+            if j < NPAIR:
+                if q == 0:
+                    grps[g] = gpool.tile([P, TPC * P, 4], BF16, align_bytes=64, name="grp")
+                scale_out(xbanks[j], grps[g][:, q * 2 * P:(q + 1) * 2 * P, :])
+                if j + 4 < NPAIR:
+                    stage_t(j + 4)
+                y32 = ypool.tile([P, 2, D], F32, name="y32")
+                eng = nc.vector if j in V_MADE else nc.gpsimd
+                eng.tensor_tensor(out=y32[:], in0=pair_rows(j), in1=w_b2, op=ALU.mult)
+                ys[j] = y32
+            if j == 0:
+                zy = ypool.tile([P, 2, D], F32, tag="y32", name="zy")
+                nc.vector.tensor_tensor(out=zy[:], in0=z_sb[:], in1=w_b2, op=ALU.mult)
+                for h in range(2):
+                    square_sum(zy, h, z2[:, h:h + 1])
+            if j == 2:
+                nc.vector.tensor_copy(out=zrep[:], in_=z2[:].unsqueeze(2).to_broadcast([P, 2, P]))
+                z2bank = psc.tile([P, 2, P], F32, tag="cr", name="z2bank")
+                for h in range(2):
+                    nc.tensor.transpose(z2bank[:, h, :], zrep[:, h, :], ident[:])
+            if j == 3:
+                nc.vector.tensor_scalar(
+                    out=nz2b[:], in0=z2bank[:].rearrange("m h r -> m (h r)"),
+                    scalar1=-0.5, scalar2=lnsig[:, 0:1], op0=ALU.mult, op1=ALU.add,
+                )
+            a = j - LAG_E1
+            if 0 <= a < NPAIR:
+                tmp = tpool.tile([P, 2, M_COLS], F32, name="tmp")
+                nc.vector.tensor_tensor(out=tmp[:], in0=crs[a][:], in1=nz2b2, op=ALU.add)
+                tmps[a] = tmp
+            b = j - LAG_E2
+            if 0 <= b < NPAIR:
+                gb, qb = divmod(b, PPC)
+                if qb == 0:
+                    outs[gb] = opool.tile([P, TPC, M_COLS], F32, name="o_sb")
+                o_sb = outs[gb]
+                for i in range(2):
+                    nc.scalar.activation(
+                        out=o_sb[:, 2 * qb + i, :], in_=tmps[b][:, i, :], func=ACT.Exp,
+                        bias=nx2[:, 2 * b + i:2 * b + i + 1], scale=1.0,
+                    )
+                dst = out[gb * CHUNK:(gb + 1) * CHUNK, :].rearrange("(p t) j -> p t j", t=TPC)
+                if gb == NCH - 1:
+                    nc.sync.dma_start(out=dst[:, 2 * qb:2 * qb + 2, :], in_=o_sb[:, 2 * qb:2 * qb + 2, :])
+                elif qb == PPC - 1:
+                    nc.sync.dma_start(out=dst, in_=o_sb[:])
+            m = j - LAG_SQ
+            if 0 <= m < NPAIR:
+                for i in range(2):
+                    square_sum(ys[m], i, x2[:, 2 * m + i:2 * m + i + 1])
+                nc.scalar.mul(out=nx2[:, 2 * m:2 * m + 2], in_=x2[:, 2 * m:2 * m + 2], mul=-0.5)
+            if j < NPAIR and q == PPC - 1:
+                xc = gpool.tile([P, TPC * P], U32, align_bytes=64, name="xc")
+                xsc = gpool.tile([P, TPC * P], U8, align_bytes=64, name="xsc")
+                nc.vector.quantize_mx(
+                    out=xc[:].bitcast(FP8X4), scales=xsc[:], in_=grps[g][:].rearrange("p c t -> p (c t)")
+                )
+                for qq in range(PPC):
+                    cr = psc.tile([P, 2, M_COLS], F32, tag="cr", name="cr")
+                    for i in range(2):
+                        cols = slice((2 * qq + i) * P, (2 * qq + i + 1) * P)
+                        nc.tensor.matmul_mx(
+                            out=cr[:, i, :],
+                            lhsT=xc[:, cols].bitcast(FP8X4), lhsT_scale=xsc[:, cols],
+                            rhs=zc[:].bitcast(FP8X4), rhs_scale=zsc[:],
+                            start=True, stop=True,
+                        )
+                    crs[g * PPC + qq] = cr

@@ -23,7 +23,7 @@ NCH = N_ROWS // CHUNK
 NPAIR = NCH * PPC
 FLOPS = 2 * N_ROWS * M_COLS * D
 
-V_MADE = (5, 13, 21, 29)
+V_MADE = (3, 7, 15, 19, 27, 31)
 LAG_E1 = 4
 LAG_E2 = 5
 LAG_SQ = 2
@@ -35,12 +35,13 @@ def tile_rbf_kernel_t_kernel(tc, X, Z, l_raw, sigma_f_raw, out):
         const = ctx.enter_context(tc.tile_pool(name="const", bufs=1))
         xpool = ctx.enter_context(tc.tile_pool(name="xpool", bufs=NCH))
         gpool = ctx.enter_context(tc.tile_pool(name="gpool", bufs=2))
-        ypool = ctx.enter_context(tc.tile_pool(name="ypool", bufs=5))
+        ypool = ctx.enter_context(tc.tile_pool(name="ypool", bufs=8))
         jpool = ctx.enter_context(tc.tile_pool(name="jpool", bufs=2))
-        tpool = ctx.enter_context(tc.tile_pool(name="tpool", bufs=4))
+        tpool = ctx.enter_context(tc.tile_pool(name="tpool", bufs=6))
         opool = ctx.enter_context(tc.tile_pool(name="opool", bufs=3))
         psx = ctx.enter_context(tc.psum_pool(name="psx", bufs=4))
-        psc = ctx.enter_context(tc.psum_pool(name="psc", bufs=4))
+        psc = ctx.enter_context(tc.psum_pool(name="psc", bufs=3))
+        psw = ctx.enter_context(tc.psum_pool(name="psw", bufs=1))
         ctx.enter_context(tc.manual_schedule())
 
         small = const.tile([P, 32], BF16)
@@ -112,7 +113,7 @@ def tile_rbf_kernel_t_kernel(tc, X, Z, l_raw, sigma_f_raw, out):
         transposes([z_sb[:, 0, :], z_sb[:, 1, :]], zbank)
         rep = const.tile([P, 4, P], F32)
         nc.vector.tensor_copy(out=rep[:], in_=w4[:].unsqueeze(2).to_broadcast([P, 4, P]))
-        wbank = psc.tile([P, 4, P], F32, tag="cr", name="wbank")
+        wbank = psw.tile([P, 4, P], F32, name="wbank")
         for t in range(4):
             nc.tensor.transpose(wbank[:, t, :], rep[:, t, :], ident[:])
         for j in range(4):
@@ -124,7 +125,18 @@ def tile_rbf_kernel_t_kernel(tc, X, Z, l_raw, sigma_f_raw, out):
             out=w_b[:].rearrange("m (u p e) -> m u p e", u=2, e=2),
             in_=wbank[:].rearrange("m (u e) p -> m u p e", u=2),
         )
-        w_b2 = w_b[:].unsqueeze(1).to_broadcast([P, 2, D])
+        w_ps = wbank[:].rearrange("m (u e) p -> m u p e", u=2)
+
+        def times_w(y32, rows, on_vector):
+            for i in range(2):
+                if on_vector:
+                    nc.vector.tensor_tensor(
+                        out=y32[:, i, :].rearrange("m (u p e) -> m u p e", u=2, e=2),
+                        in0=rows[:, i, :].rearrange("m (u p e) -> m u p e", u=2, e=2),
+                        in1=w_ps, op=ALU.mult,
+                    )
+                else:
+                    nc.gpsimd.tensor_tensor(out=y32[:, i, :], in0=rows[:, i, :], in1=w_b[:], op=ALU.mult)
         zc = const.tile([P, 2 * P], U32, align_bytes=64)
         zsc = const.tile([P, 2 * P], U8, align_bytes=64)
         nc.vector.quantize_mx(
@@ -149,6 +161,20 @@ def tile_rbf_kernel_t_kernel(tc, X, Z, l_raw, sigma_f_raw, out):
         tmps = {}
         outs = {}
 
+        def cross(pair):
+            gg, qq = divmod(pair, PPC)
+            xc, xsc = quant[gg]
+            cr = psc.tile([P, 2, M_COLS], F32, tag="cr", name="cr")
+            for i in range(2):
+                cols = slice((2 * qq + i) * P, (2 * qq + i + 1) * P)
+                nc.tensor.matmul_mx(
+                    out=cr[:, i, :],
+                    lhsT=xc[:, cols].bitcast(FP8X4), lhsT_scale=xsc[:, cols],
+                    rhs=zc[:].bitcast(FP8X4), rhs_scale=zsc[:],
+                    start=True, stop=True,
+                )
+            crs[pair] = cr
+
         for j in range(NPAIR + LAG_E2 + 1):
             g, q = divmod(j, PPC)
             if j < NPAIR:
@@ -158,12 +184,11 @@ def tile_rbf_kernel_t_kernel(tc, X, Z, l_raw, sigma_f_raw, out):
                 if j + 4 < NPAIR:
                     stage_t(j + 4)
                 y32 = ypool.tile([P, 2, D], F32, name="y32")
-                eng = nc.vector if j in V_MADE else nc.gpsimd
-                eng.tensor_tensor(out=y32[:], in0=pair_rows(j), in1=w_b2, op=ALU.mult)
+                times_w(y32, pair_rows(j), j in V_MADE)
                 ys[j] = y32
             if j == 0:
                 zy = ypool.tile([P, 2, D], F32, tag="y32", name="zy")
-                nc.vector.tensor_tensor(out=zy[:], in0=z_sb[:], in1=w_b2, op=ALU.mult)
+                times_w(zy, z_sb[:], True)
                 for h in range(2):
                     square_sum(zy, h, z2[:, h:h + 1])
             if j == 2:
@@ -181,6 +206,8 @@ def tile_rbf_kernel_t_kernel(tc, X, Z, l_raw, sigma_f_raw, out):
                 tmp = tpool.tile([P, 2, M_COLS], F32, name="tmp")
                 nc.vector.tensor_tensor(out=tmp[:], in0=crs[a][:], in1=nz2b2, op=ALU.add)
                 tmps[a] = tmp
+                if a % PPC == 0:
+                    cross(a + PPC - 1)
             b = j - LAG_E2
             if 0 <= b < NPAIR:
                 gb, qb = divmod(b, PPC)
@@ -208,14 +235,6 @@ def tile_rbf_kernel_t_kernel(tc, X, Z, l_raw, sigma_f_raw, out):
                 nc.vector.quantize_mx(
                     out=xc[:].bitcast(FP8X4), scales=xsc[:], in_=grps[g][:].rearrange("p c t -> p (c t)")
                 )
-                for qq in range(PPC):
-                    cr = psc.tile([P, 2, M_COLS], F32, tag="cr", name="cr")
-                    for i in range(2):
-                        cols = slice((2 * qq + i) * P, (2 * qq + i + 1) * P)
-                        nc.tensor.matmul_mx(
-                            out=cr[:, i, :],
-                            lhsT=xc[:, cols].bitcast(FP8X4), lhsT_scale=xsc[:, cols],
-                            rhs=zc[:].bitcast(FP8X4), rhs_scale=zsc[:],
-                            start=True, stop=True,
-                        )
-                    crs[g * PPC + qq] = cr
+                quant[g] = (xc, xsc)
+                for qq in range(PPC - 1):
+                    cross(g * PPC + qq)

@@ -1,3 +1,4 @@
+import math
 from contextlib import ExitStack
 
 import concourse.mybir as mybir
@@ -23,10 +24,11 @@ NCH = N_ROWS // CHUNK
 NPAIR = NCH * PPC
 FLOPS = 2 * N_ROWS * M_COLS * D
 
-V_MADE = (3, 7, 15, 19, 27, 31)
+XT_BANKS = 3
+LEAD_SQ = 1
+LAG_RED = 3
 LAG_E1 = 4
 LAG_E2 = 5
-LAG_SQ = 2
 
 
 def tile_rbf_kernel_t_kernel(tc, X, Z, l_raw, sigma_f_raw, out):
@@ -35,13 +37,13 @@ def tile_rbf_kernel_t_kernel(tc, X, Z, l_raw, sigma_f_raw, out):
         const = ctx.enter_context(tc.tile_pool(name="const", bufs=1))
         xpool = ctx.enter_context(tc.tile_pool(name="xpool", bufs=NCH))
         gpool = ctx.enter_context(tc.tile_pool(name="gpool", bufs=2))
-        ypool = ctx.enter_context(tc.tile_pool(name="ypool", bufs=8))
-        jpool = ctx.enter_context(tc.tile_pool(name="jpool", bufs=2))
+        spool = ctx.enter_context(tc.tile_pool(name="spool", bufs=4))
         tpool = ctx.enter_context(tc.tile_pool(name="tpool", bufs=6))
+        jpool = ctx.enter_context(tc.tile_pool(name="jpool", bufs=2))
         opool = ctx.enter_context(tc.tile_pool(name="opool", bufs=3))
-        psx = ctx.enter_context(tc.psum_pool(name="psx", bufs=4))
+        psx = ctx.enter_context(tc.psum_pool(name="psx", bufs=XT_BANKS))
         psc = ctx.enter_context(tc.psum_pool(name="psc", bufs=3))
-        psw = ctx.enter_context(tc.psum_pool(name="psw", bufs=1))
+        psa = ctx.enter_context(tc.psum_pool(name="psa", bufs=2))
         ctx.enter_context(tc.manual_schedule())
 
         small = const.tile([P, 32], BF16)
@@ -66,21 +68,6 @@ def tile_rbf_kernel_t_kernel(tc, X, Z, l_raw, sigma_f_raw, out):
         ident = const.tile([P, P], F32)
         make_identity(nc, ident[:])
 
-        capped = const.tile([P, 32], F32)
-        nc.vector.tensor_scalar_min(out=capped[:], in0=small[:], scalar1=LIM)
-        expv = const.tile([P, 32], F32)
-        nc.scalar.activation(out=expv[:], in_=capped[:], func=ACT.Exp)
-        logv = const.tile([P, 32], F32)
-        nc.scalar.activation(out=logv[:], in_=expv[:], func=ACT.Ln, bias=1.0)
-        splus = const.tile([P, 32], F32)
-        nc.vector.tensor_tensor(out=splus[:], in0=logv[:], in1=small[:], op=ALU.max)
-        w4 = const.tile([P, 4], F32)
-        nc.vector.reciprocal(out=w4[:], in_=splus[:, 0:4])
-        lnsig = const.tile([P, 1], F32)
-        nc.scalar.activation(out=lnsig[:], in_=splus[:, 16:17], func=ACT.Ln)
-
-        w4_b = w4[:].rearrange("p (o u e) -> p o u e", o=1, u=2).to_broadcast([P, 2 * P, 2, 2])
-
         def transposes(src_pair, bank):
             for i, src in enumerate(src_pair):
                 words = src.bitcast(F32)
@@ -88,14 +75,6 @@ def tile_rbf_kernel_t_kernel(tc, X, Z, l_raw, sigma_f_raw, out):
                     nc.tensor.transpose(
                         bank[:, u, i * P:(i + 1) * P], words[:, u * P:(u + 1) * P], ident[:]
                     )
-
-        def scale_out(bank, grouped):
-            nc.vector.tensor_tensor(
-                out=grouped.rearrange("p c (u e) -> p c u e", u=2),
-                in0=bank[:].bitcast(BF16).rearrange("p u (c e) -> p c u e", e=2),
-                in1=w4_b,
-                op=ALU.mult,
-            )
 
         def pair_rows(j):
             c, q = divmod(j, PPC)
@@ -109,57 +88,96 @@ def tile_rbf_kernel_t_kernel(tc, X, Z, l_raw, sigma_f_raw, out):
             transposes([rows[:, 0, :], rows[:, 1, :]], bank)
             xbanks[j] = bank
 
+        def raw_squares(bank):
+            sq = spool.tile([P, 4, 2 * P], F32, name="sq")
+            nc.scalar.activation(
+                out=sq[:].rearrange("p (u e) c -> p u c e", u=2),
+                in_=bank[:].bitcast(BF16).rearrange("p u (c e) -> p u c e", e=2),
+                func=ACT.Square,
+            )
+            return sq
+
+        def squares(bank):
+            sq = spool.tile([P, 4, 2 * P], F32, name="sq")
+            halves = bank[:].bitcast(BF16).rearrange("p u (c e) -> p u c e", e=2)
+            for u in range(2):
+                for e in range(2):
+                    t = 2 * u + e
+                    nc.scalar.activation(
+                        out=sq[:, t, :], in_=halves[:, u, :, e], func=ACT.Square, scale=w4h[:, t:t + 1]
+                    )
+            return sq
+
         zbank = psc.tile([P, 2, 2 * P], F32, tag="cr", name="zbank")
         transposes([z_sb[:, 0, :], z_sb[:, 1, :]], zbank)
-        rep = const.tile([P, 4, P], F32)
-        nc.vector.tensor_copy(out=rep[:], in_=w4[:].unsqueeze(2).to_broadcast([P, 4, P]))
-        wbank = psw.tile([P, 4, P], F32, name="wbank")
-        for t in range(4):
-            nc.tensor.transpose(wbank[:, t, :], rep[:, t, :], ident[:])
-        for j in range(4):
+        for j in range(XT_BANKS):
             stage_t(j)
+
+        capped = const.tile([P, 32], F32)
+        nc.vector.tensor_scalar_min(out=capped[:], in0=small[:], scalar1=LIM)
+        expv = const.tile([P, 32], F32)
+        nc.scalar.activation(out=expv[:], in_=capped[:], func=ACT.Exp)
+        logv = const.tile([P, 32], F32)
+        nc.scalar.activation(out=logv[:], in_=expv[:], func=ACT.Ln, bias=1.0)
+        splus = const.tile([P, 32], F32)
+        nc.vector.tensor_tensor(out=splus[:], in0=logv[:], in1=small[:], op=ALU.max)
+        w4 = const.tile([P, 4], F32)
+        nc.vector.reciprocal(out=w4[:], in_=splus[:, 0:4])
+        w4_b = w4[:].rearrange("p (o u e) -> p o u e", o=1, u=2).to_broadcast([P, 2 * P, 2, 2])
+
+        def scale_out(bank, grouped):
+            nc.vector.tensor_tensor(
+                out=grouped.rearrange("p c (u e) -> p c u e", u=2),
+                in0=bank[:].bitcast(BF16).rearrange("p u (c e) -> p c u e", e=2),
+                in1=w4_b,
+                op=ALU.mult,
+            )
+
+        w4h = const.tile([P, 4], F32)
+        nc.vector.tensor_scalar_mul(out=w4h[:], in0=w4[:], scalar1=math.sqrt(0.5))
+        sqz = raw_squares(zbank)
+        sqs = {0: squares(xbanks[0])}
+        lnsig = const.tile([P, 1], F32)
+        nc.scalar.activation(out=lnsig[:], in_=splus[:, 16:17], func=ACT.Ln)
+
+        nw2 = const.tile([P, 4], F32)
+        nc.vector.scalar_tensor_tensor(
+            out=nw2[:], in0=w4[:], scalar=-0.5, in1=w4[:], op0=ALU.mult, op1=ALU.mult
+        )
         zgrp = const.tile([P, 2 * P, 4], BF16, align_bytes=64)
         scale_out(zbank, zgrp[:])
-        w_b = const.tile([P, D], F32)
-        nc.vector.tensor_copy(
-            out=w_b[:].rearrange("m (u p e) -> m u p e", u=2, e=2),
-            in_=wbank[:].rearrange("m (u e) p -> m u p e", u=2),
-        )
-        w_ps = wbank[:].rearrange("m (u e) p -> m u p e", u=2)
 
-        def times_w(y32, rows, on_vector):
-            for i in range(2):
-                if on_vector:
-                    nc.vector.tensor_tensor(
-                        out=y32[:, i, :].rearrange("m (u p e) -> m u p e", u=2, e=2),
-                        in0=rows[:, i, :].rearrange("m (u p e) -> m u p e", u=2, e=2),
-                        in1=w_ps, op=ALU.mult,
-                    )
-                else:
-                    nc.gpsimd.tensor_tensor(out=y32[:, i, :], in0=rows[:, i, :], in1=w_b[:], op=ALU.mult)
+        z2bank = psc.tile([P, M_COLS], F32, tag="cr", name="z2bank")
+        for t in range(4):
+            nc.tensor.matmul(
+                out=z2bank[:], lhsT=nw2[:, t:t + 1].to_broadcast([P, P]), rhs=sqz[:, t, :],
+                start=(t == 0), stop=(t == 3),
+            )
+
         zc = const.tile([P, 2 * P], U32, align_bytes=64)
         zsc = const.tile([P, 2 * P], U8, align_bytes=64)
-        nc.vector.quantize_mx(
-            out=zc[:].bitcast(FP8X4), scales=zsc[:], in_=zgrp[:].rearrange("p c t -> p (c t)")
-        )
-
-        z2 = const.tile([P, 2], F32)
-        zrep = const.tile([P, 2, P], F32)
         nz2b = const.tile([P, M_COLS], F32)
         nz2b2 = nz2b[:].unsqueeze(1).to_broadcast([P, 2, M_COLS])
-        x2 = const.tile([P, 2 * NPAIR], F32)
+        x2h = const.tile([P, 2 * NPAIR], F32)
         nx2 = const.tile([P, 2 * NPAIR], F32)
 
-        def square_sum(y32, i, acc):
-            junk = jpool.tile([P, D], BF16, name="junk")
-            nc.scalar.activation(out=junk[:], in_=y32[:, i, :], func=ACT.Square, accum_out=acc)
-
-        ys = {}
         grps = {}
         quant = {}
         crs = {}
         tmps = {}
         outs = {}
+        accs = {}
+
+        def norms(pair):
+            r, half = divmod(pair, 2)
+            if half == 0:
+                accs[r] = psa.tile([P, 4, P], F32, name="acc")
+            for i in range(2):
+                for t in range(4):
+                    nc.tensor.matmul(
+                        out=accs[r][:, 2 * half + i, :], lhsT=sqs[pair][:, t, i * P:(i + 1) * P], rhs=ident[:],
+                        is_transpose=True, start=(t == 0), stop=(t == 3),
+                    )
 
         def cross(pair):
             gg, qq = divmod(pair, PPC)
@@ -178,29 +196,26 @@ def tile_rbf_kernel_t_kernel(tc, X, Z, l_raw, sigma_f_raw, out):
         for j in range(NPAIR + LAG_E2 + 1):
             g, q = divmod(j, PPC)
             if j < NPAIR:
+                norms(j)
+                if j + LEAD_SQ < NPAIR:
+                    sqs[j + LEAD_SQ] = squares(xbanks[j + LEAD_SQ])
                 if q == 0:
                     grps[g] = gpool.tile([P, TPC * P, 4], BF16, align_bytes=64, name="grp")
                 scale_out(xbanks[j], grps[g][:, q * 2 * P:(q + 1) * 2 * P, :])
-                if j + 4 < NPAIR:
-                    stage_t(j + 4)
-                y32 = ypool.tile([P, 2, D], F32, name="y32")
-                times_w(y32, pair_rows(j), j in V_MADE)
-                ys[j] = y32
+                if j + XT_BANKS < NPAIR:
+                    stage_t(j + XT_BANKS)
+            if (j - LAG_RED) % 2 == 0 and 0 <= (j - LAG_RED) // 2 < NPAIR // 2:
+                r = (j - LAG_RED) // 2
+                if r % 2 == 0:
+                    nc.vector.tensor_reduce(
+                        out=x2h[:, 4 * r:4 * r + 4], in_=accs[r][:], axis=mybir.AxisListType.X, op=ALU.add
+                    )
             if j == 0:
-                zy = ypool.tile([P, 2, D], F32, tag="y32", name="zy")
-                times_w(zy, z_sb[:], True)
-                for h in range(2):
-                    square_sum(zy, h, z2[:, h:h + 1])
-            if j == 2:
-                nc.vector.tensor_copy(out=zrep[:], in_=z2[:].unsqueeze(2).to_broadcast([P, 2, P]))
-                z2bank = psc.tile([P, 2, P], F32, tag="cr", name="z2bank")
-                for h in range(2):
-                    nc.tensor.transpose(z2bank[:, h, :], zrep[:, h, :], ident[:])
-            if j == 3:
-                nc.vector.tensor_scalar(
-                    out=nz2b[:], in0=z2bank[:].rearrange("m h r -> m (h r)"),
-                    scalar1=-0.5, scalar2=lnsig[:, 0:1], op0=ALU.mult, op1=ALU.add,
+                nc.vector.quantize_mx(
+                    out=zc[:].bitcast(FP8X4), scales=zsc[:], in_=zgrp[:].rearrange("p c t -> p (c t)")
                 )
+            if j == 1:
+                nc.vector.tensor_scalar_add(out=nz2b[:], in0=z2bank[:], scalar1=lnsig[:, 0:1])
             a = j - LAG_E1
             if 0 <= a < NPAIR:
                 tmp = tpool.tile([P, 2, M_COLS], F32, name="tmp")
@@ -224,11 +239,19 @@ def tile_rbf_kernel_t_kernel(tc, X, Z, l_raw, sigma_f_raw, out):
                     nc.sync.dma_start(out=dst[:, 2 * qb:2 * qb + 2, :], in_=o_sb[:, 2 * qb:2 * qb + 2, :])
                 elif qb == PPC - 1:
                     nc.sync.dma_start(out=dst, in_=o_sb[:])
-            m = j - LAG_SQ
-            if 0 <= m < NPAIR:
-                for i in range(2):
-                    square_sum(ys[m], i, x2[:, 2 * m + i:2 * m + i + 1])
-                nc.scalar.mul(out=nx2[:, 2 * m:2 * m + 2], in_=x2[:, 2 * m:2 * m + 2], mul=-0.5)
+            if (j - LAG_RED - 1) % 2 == 0 and 0 <= (j - LAG_RED - 1) // 2 < NPAIR // 2:
+                r = (j - LAG_RED - 1) // 2
+                if r % 2 == 0:
+                    nc.scalar.mul(out=nx2[:, 4 * r:4 * r + 4], in_=x2h[:, 4 * r:4 * r + 4], mul=-1.0)
+            if (j - LAG_RED) % 2 == 0 and 0 <= (j - LAG_RED) // 2 < NPAIR // 2:
+                r = (j - LAG_RED) // 2
+                if r % 2 == 1:
+                    for slot in range(4):
+                        junk = jpool.tile([P, P], BF16, name="junk")
+                        nc.scalar.activation(
+                            out=junk[:], in_=accs[r][:, slot, :], func=ACT.Identity, scale=-1.0,
+                            accum_out=nx2[:, 4 * r + slot:4 * r + slot + 1],
+                        )
             if j < NPAIR and q == PPC - 1:
                 xc = gpool.tile([P, TPC * P], U32, align_bytes=64, name="xc")
                 xsc = gpool.tile([P, TPC * P], U8, align_bytes=64, name="xsc")

@@ -25,8 +25,7 @@ NPAIR = NCH * PPC
 FLOPS = 2 * N_ROWS * M_COLS * D
 
 XT_BANKS = 3
-LEAD_SQ = 1
-LAG_RED = 3
+LAG_RED = 4
 LAG_E1 = 4
 LAG_E2 = 5
 
@@ -88,15 +87,6 @@ def tile_rbf_kernel_t_kernel(tc, X, Z, l_raw, sigma_f_raw, out):
             transposes([rows[:, 0, :], rows[:, 1, :]], bank)
             xbanks[j] = bank
 
-        def raw_squares(bank):
-            sq = spool.tile([P, 4, 2 * P], F32, name="sq")
-            nc.scalar.activation(
-                out=sq[:].rearrange("p (u e) c -> p u c e", u=2),
-                in_=bank[:].bitcast(BF16).rearrange("p u (c e) -> p u c e", e=2),
-                func=ACT.Square,
-            )
-            return sq
-
         def squares(bank):
             sq = spool.tile([P, 4, 2 * P], F32, name="sq")
             halves = bank[:].bitcast(BF16).rearrange("p u (c e) -> p u c e", e=2)
@@ -135,24 +125,25 @@ def tile_rbf_kernel_t_kernel(tc, X, Z, l_raw, sigma_f_raw, out):
 
         w4h = const.tile([P, 4], F32)
         nc.vector.tensor_scalar_mul(out=w4h[:], in0=w4[:], scalar1=math.sqrt(0.5))
-        sqz = raw_squares(zbank)
-        sqs = {0: squares(xbanks[0])}
+        zgrp = const.tile([P, 2 * P, 4], BF16, align_bytes=64)
+        scale_out(zbank, zgrp[:])
+        sqz = squares(zbank)
+        sqs = {}
         lnsig = const.tile([P, 1], F32)
         nc.scalar.activation(out=lnsig[:], in_=splus[:, 16:17], func=ACT.Ln)
 
-        nw2 = const.tile([P, 4], F32)
-        nc.vector.scalar_tensor_tensor(
-            out=nw2[:], in0=w4[:], scalar=-0.5, in1=w4[:], op0=ALU.mult, op1=ALU.mult
-        )
-        zgrp = const.tile([P, 2 * P, 4], BF16, align_bytes=64)
-        scale_out(zbank, zgrp[:])
+        def add_planes(sq, i, dst):
+            for t in range(4):
+                nc.tensor.matmul(
+                    out=dst, lhsT=sq[:, t, i * P:(i + 1) * P], rhs=ident[:],
+                    is_transpose=True, start=(t == 0), stop=(t == 3),
+                )
 
-        z2bank = psc.tile([P, M_COLS], F32, tag="cr", name="z2bank")
-        for t in range(4):
-            nc.tensor.matmul(
-                out=z2bank[:], lhsT=nw2[:, t:t + 1].to_broadcast([P, P]), rhs=sqz[:, t, :],
-                start=(t == 0), stop=(t == 3),
-            )
+        accz = psa.tile([P, 2, P], F32, tag="acc", name="accz")
+        for h in range(2):
+            add_planes(sqz, h, accz[:, h, :])
+        z2h = const.tile([P, 2], F32)
+        zrep = const.tile([P, 2, P], F32)
 
         zc = const.tile([P, 2 * P], U32, align_bytes=64)
         zsc = const.tile([P, 2 * P], U8, align_bytes=64)
@@ -171,13 +162,9 @@ def tile_rbf_kernel_t_kernel(tc, X, Z, l_raw, sigma_f_raw, out):
         def norms(pair):
             r, half = divmod(pair, 2)
             if half == 0:
-                accs[r] = psa.tile([P, 4, P], F32, name="acc")
+                accs[r] = psa.tile([P, 4, P], F32, tag="acc", name="acc")
             for i in range(2):
-                for t in range(4):
-                    nc.tensor.matmul(
-                        out=accs[r][:, 2 * half + i, :], lhsT=sqs[pair][:, t, i * P:(i + 1) * P], rhs=ident[:],
-                        is_transpose=True, start=(t == 0), stop=(t == 3),
-                    )
+                add_planes(sqs[pair], i, accs[r][:, 2 * half + i, :])
 
         def cross(pair):
             gg, qq = divmod(pair, PPC)
@@ -195,13 +182,13 @@ def tile_rbf_kernel_t_kernel(tc, X, Z, l_raw, sigma_f_raw, out):
 
         for j in range(NPAIR + LAG_E2 + 1):
             g, q = divmod(j, PPC)
+            if 1 <= j <= NPAIR:
+                norms(j - 1)
             if j < NPAIR:
-                norms(j)
-                if j + LEAD_SQ < NPAIR:
-                    sqs[j + LEAD_SQ] = squares(xbanks[j + LEAD_SQ])
                 if q == 0:
                     grps[g] = gpool.tile([P, TPC * P, 4], BF16, align_bytes=64, name="grp")
                 scale_out(xbanks[j], grps[g][:, q * 2 * P:(q + 1) * 2 * P, :])
+                sqs[j] = squares(xbanks[j])
                 if j + XT_BANKS < NPAIR:
                     stage_t(j + XT_BANKS)
             if (j - LAG_RED) % 2 == 0 and 0 <= (j - LAG_RED) // 2 < NPAIR // 2:
@@ -215,7 +202,16 @@ def tile_rbf_kernel_t_kernel(tc, X, Z, l_raw, sigma_f_raw, out):
                     out=zc[:].bitcast(FP8X4), scales=zsc[:], in_=zgrp[:].rearrange("p c t -> p (c t)")
                 )
             if j == 1:
-                nc.vector.tensor_scalar_add(out=nz2b[:], in0=z2bank[:], scalar1=lnsig[:, 0:1])
+                nc.vector.tensor_reduce(out=z2h[:], in_=accz[:], axis=mybir.AxisListType.X, op=ALU.add)
+                nc.vector.tensor_scalar(
+                    out=zrep[:], in0=z2h[:].unsqueeze(2).to_broadcast([P, 2, P]),
+                    scalar1=-1.0, scalar2=lnsig[:, 0:1], op0=ALU.mult, op1=ALU.add,
+                )
+                z2bank = psc.tile([P, 2, P], F32, tag="cr", name="z2bank")
+                for h in range(2):
+                    nc.tensor.transpose(z2bank[:, h, :], zrep[:, h, :], ident[:])
+            if j == 3:
+                nc.vector.tensor_copy(out=nz2b[:], in_=z2bank[:].rearrange("m h r -> m (h r)"))
             a = j - LAG_E1
             if 0 <= a < NPAIR:
                 tmp = tpool.tile([P, 2, M_COLS], F32, name="tmp")
@@ -239,8 +235,8 @@ def tile_rbf_kernel_t_kernel(tc, X, Z, l_raw, sigma_f_raw, out):
                     nc.sync.dma_start(out=dst[:, 2 * qb:2 * qb + 2, :], in_=o_sb[:, 2 * qb:2 * qb + 2, :])
                 elif qb == PPC - 1:
                     nc.sync.dma_start(out=dst, in_=o_sb[:])
-            if (j - LAG_RED - 1) % 2 == 0 and 0 <= (j - LAG_RED - 1) // 2 < NPAIR // 2:
-                r = (j - LAG_RED - 1) // 2
+            if (j - LAG_RED) % 2 == 0 and 0 <= (j - LAG_RED) // 2 < NPAIR // 2:
+                r = (j - LAG_RED) // 2
                 if r % 2 == 0:
                     nc.scalar.mul(out=nx2[:, 4 * r:4 * r + 4], in_=x2h[:, 4 * r:4 * r + 4], mul=-1.0)
             if (j - LAG_RED) % 2 == 0 and 0 <= (j - LAG_RED) // 2 < NPAIR // 2:

@@ -25,7 +25,11 @@ NPAIR = NCH * PPC
 FLOPS = 2 * N_ROWS * M_COLS * D
 
 XT_BANKS = 3
-LAG_RED = 4
+LEAD_SQ = 1
+LAG_RED = 2
+G_PAIRS = tuple(range(5, NPAIR, PPC))
+B_PAIRS = tuple(j for j in range(NPAIR) if j not in G_PAIRS)
+N_ACC = (len(B_PAIRS) + 1) // 2
 LAG_E1 = 4
 LAG_E2 = 5
 
@@ -39,6 +43,7 @@ def tile_rbf_kernel_t_kernel(tc, X, Z, l_raw, sigma_f_raw, out):
         spool = ctx.enter_context(tc.tile_pool(name="spool", bufs=4))
         tpool = ctx.enter_context(tc.tile_pool(name="tpool", bufs=6))
         jpool = ctx.enter_context(tc.tile_pool(name="jpool", bufs=2))
+        ypool = ctx.enter_context(tc.tile_pool(name="ypool", bufs=1))
         opool = ctx.enter_context(tc.tile_pool(name="opool", bufs=3))
         psx = ctx.enter_context(tc.psum_pool(name="psx", bufs=XT_BANKS))
         psc = ctx.enter_context(tc.psum_pool(name="psc", bufs=3))
@@ -87,6 +92,15 @@ def tile_rbf_kernel_t_kernel(tc, X, Z, l_raw, sigma_f_raw, out):
             transposes([rows[:, 0, :], rows[:, 1, :]], bank)
             xbanks[j] = bank
 
+        def raw_squares(bank):
+            sq = spool.tile([P, 4, 2 * P], F32, name="sq")
+            nc.scalar.activation(
+                out=sq[:].rearrange("p (u e) c -> p u c e", u=2),
+                in_=bank[:].bitcast(BF16).rearrange("p u (c e) -> p u c e", e=2),
+                func=ACT.Square,
+            )
+            return sq
+
         def squares(bank):
             sq = spool.tile([P, 4, 2 * P], F32, name="sq")
             halves = bank[:].bitcast(BF16).rearrange("p u (c e) -> p u c e", e=2)
@@ -125,32 +139,62 @@ def tile_rbf_kernel_t_kernel(tc, X, Z, l_raw, sigma_f_raw, out):
 
         w4h = const.tile([P, 4], F32)
         nc.vector.tensor_scalar_mul(out=w4h[:], in0=w4[:], scalar1=math.sqrt(0.5))
-        zgrp = const.tile([P, 2 * P, 4], BF16, align_bytes=64)
-        scale_out(zbank, zgrp[:])
-        sqz = squares(zbank)
-        sqs = {}
+        sqz = raw_squares(zbank)
+        sqs = {0: squares(xbanks[0])}
         lnsig = const.tile([P, 1], F32)
         nc.scalar.activation(out=lnsig[:], in_=splus[:, 16:17], func=ACT.Ln)
 
-        def add_planes(sq, i, dst):
-            for t in range(4):
-                nc.tensor.matmul(
-                    out=dst, lhsT=sq[:, t, i * P:(i + 1) * P], rhs=ident[:],
-                    is_transpose=True, start=(t == 0), stop=(t == 3),
-                )
+        nw2 = const.tile([P, 4], F32)
+        nc.vector.scalar_tensor_tensor(
+            out=nw2[:], in0=w4[:], scalar=-0.5, in1=w4[:], op0=ALU.mult, op1=ALU.mult
+        )
+        zgrp = const.tile([P, 2 * P, 4], BF16, align_bytes=64)
+        scale_out(zbank, zgrp[:])
+        rep = const.tile([P, 4, P], F32)
+        nc.vector.tensor_copy(out=rep[:], in_=w4[:].unsqueeze(2).to_broadcast([P, 4, P]))
+        wbank = psc.tile([P, 4, P], F32, tag="cr", name="wbank")
+        for t in range(4):
+            nc.tensor.transpose(wbank[:, t, :], rep[:, t, :], ident[:])
+        w_b = const.tile([P, D], F32)
+        w_b2 = w_b[:].unsqueeze(1).to_broadcast([P, 2, D])
 
-        accz = psa.tile([P, 2, P], F32, tag="acc", name="accz")
-        for h in range(2):
-            add_planes(sqz, h, accz[:, h, :])
-        z2h = const.tile([P, 2], F32)
-        zrep = const.tile([P, 2, P], F32)
+        z2bank = psc.tile([P, M_COLS], F32, tag="cr", name="z2bank")
+        for t in range(4):
+            nc.tensor.matmul(
+                out=z2bank[:], lhsT=nw2[:, t:t + 1].to_broadcast([P, P]), rhs=sqz[:, t, :],
+                start=(t == 0), stop=(t == 3),
+            )
 
         zc = const.tile([P, 2 * P], U32, align_bytes=64)
         zsc = const.tile([P, 2 * P], U8, align_bytes=64)
+        nc.vector.quantize_mx(
+            out=zc[:].bitcast(FP8X4), scales=zsc[:], in_=zgrp[:].rearrange("p c t -> p (c t)")
+        )
         nz2b = const.tile([P, M_COLS], F32)
         nz2b2 = nz2b[:].unsqueeze(1).to_broadcast([P, 2, M_COLS])
-        x2h = const.tile([P, 2 * NPAIR], F32)
-        nx2 = const.tile([P, 2 * NPAIR], F32)
+        x2h = const.tile([P, 4 * N_ACC], F32)
+        nx2 = const.tile([P, 4 * N_ACC], F32)
+        x2g = const.tile([P, 2 * len(G_PAIRS)], F32)
+        nx2g = const.tile([P, 2 * len(G_PAIRS)], F32)
+
+        def bias_of(pair, i):
+            if pair in G_PAIRS:
+                col = 2 * G_PAIRS.index(pair) + i
+                return nx2g[:, col:col + 1]
+            col = 2 * B_PAIRS.index(pair) + i
+            return nx2[:, col:col + 1]
+
+        def natural_norms(pair):
+            y32 = ypool.tile([P, 2, D], F32, name="y32")
+            nc.gpsimd.tensor_tensor(out=y32[:], in0=pair_rows(pair), in1=w_b2, op=ALU.mult)
+            col = 2 * G_PAIRS.index(pair)
+            for i in range(2):
+                junk = jpool.tile([P, D], BF16, tag="junkw", name="junkw")
+                nc.scalar.activation(
+                    out=junk[:], in_=y32[:, i, :], func=ACT.Square, scale=math.sqrt(0.5),
+                    accum_out=x2g[:, col + i:col + i + 1],
+                )
+            nc.scalar.mul(out=nx2g[:, col:col + 2], in_=x2g[:, col:col + 2], mul=-1.0)
 
         grps = {}
         quant = {}
@@ -160,11 +204,15 @@ def tile_rbf_kernel_t_kernel(tc, X, Z, l_raw, sigma_f_raw, out):
         accs = {}
 
         def norms(pair):
-            r, half = divmod(pair, 2)
+            r, half = divmod(B_PAIRS.index(pair), 2)
             if half == 0:
-                accs[r] = psa.tile([P, 4, P], F32, tag="acc", name="acc")
+                accs[r] = psa.tile([P, 4, P], F32, name="acc")
             for i in range(2):
-                add_planes(sqs[pair], i, accs[r][:, 2 * half + i, :])
+                for t in range(4):
+                    nc.tensor.matmul(
+                        out=accs[r][:, 2 * half + i, :], lhsT=sqs[pair][:, t, i * P:(i + 1) * P], rhs=ident[:],
+                        is_transpose=True, start=(t == 0), stop=(t == 3),
+                    )
 
         def cross(pair):
             gg, qq = divmod(pair, PPC)
@@ -182,36 +230,33 @@ def tile_rbf_kernel_t_kernel(tc, X, Z, l_raw, sigma_f_raw, out):
 
         for j in range(NPAIR + LAG_E2 + 1):
             g, q = divmod(j, PPC)
-            if 1 <= j <= NPAIR:
-                norms(j - 1)
             if j < NPAIR:
+                if j in B_PAIRS:
+                    norms(j)
+                if j + LEAD_SQ < NPAIR:
+                    if j + LEAD_SQ in G_PAIRS:
+                        natural_norms(j + LEAD_SQ)
+                    else:
+                        sqs[j + LEAD_SQ] = squares(xbanks[j + LEAD_SQ])
                 if q == 0:
                     grps[g] = gpool.tile([P, TPC * P, 4], BF16, align_bytes=64, name="grp")
                 scale_out(xbanks[j], grps[g][:, q * 2 * P:(q + 1) * 2 * P, :])
-                sqs[j] = squares(xbanks[j])
                 if j + XT_BANKS < NPAIR:
                     stage_t(j + XT_BANKS)
-            if (j - LAG_RED) % 2 == 0 and 0 <= (j - LAG_RED) // 2 < NPAIR // 2:
-                r = (j - LAG_RED) // 2
-                if r % 2 == 0:
+            due = [r for r in range(N_ACC) if B_PAIRS[min(2 * r + 1, len(B_PAIRS) - 1)] + LAG_RED == j]
+            for r in due:
+                n = min(4, 2 * len(B_PAIRS) - 4 * r)
+                if r % 3 != 1:
                     nc.vector.tensor_reduce(
-                        out=x2h[:, 4 * r:4 * r + 4], in_=accs[r][:], axis=mybir.AxisListType.X, op=ALU.add
+                        out=x2h[:, 4 * r:4 * r + n], in_=accs[r][:, 0:n, :], axis=mybir.AxisListType.X, op=ALU.add
                     )
             if j == 0:
-                nc.vector.quantize_mx(
-                    out=zc[:].bitcast(FP8X4), scales=zsc[:], in_=zgrp[:].rearrange("p c t -> p (c t)")
+                nc.vector.tensor_copy(
+                    out=w_b[:].rearrange("m (u p e) -> m u p e", u=2, e=2),
+                    in_=wbank[:].rearrange("m (u e) p -> m u p e", u=2),
                 )
             if j == 1:
-                nc.vector.tensor_reduce(out=z2h[:], in_=accz[:], axis=mybir.AxisListType.X, op=ALU.add)
-                nc.vector.tensor_scalar(
-                    out=zrep[:], in0=z2h[:].unsqueeze(2).to_broadcast([P, 2, P]),
-                    scalar1=-1.0, scalar2=lnsig[:, 0:1], op0=ALU.mult, op1=ALU.add,
-                )
-                z2bank = psc.tile([P, 2, P], F32, tag="cr", name="z2bank")
-                for h in range(2):
-                    nc.tensor.transpose(z2bank[:, h, :], zrep[:, h, :], ident[:])
-            if j == 3:
-                nc.vector.tensor_copy(out=nz2b[:], in_=z2bank[:].rearrange("m h r -> m (h r)"))
+                nc.vector.tensor_scalar_add(out=nz2b[:], in0=z2bank[:], scalar1=lnsig[:, 0:1])
             a = j - LAG_E1
             if 0 <= a < NPAIR:
                 tmp = tpool.tile([P, 2, M_COLS], F32, name="tmp")
@@ -228,21 +273,19 @@ def tile_rbf_kernel_t_kernel(tc, X, Z, l_raw, sigma_f_raw, out):
                 for i in range(2):
                     nc.scalar.activation(
                         out=o_sb[:, 2 * qb + i, :], in_=tmps[b][:, i, :], func=ACT.Exp,
-                        bias=nx2[:, 2 * b + i:2 * b + i + 1], scale=1.0,
+                        bias=bias_of(b, i), scale=1.0,
                     )
                 dst = out[gb * CHUNK:(gb + 1) * CHUNK, :].rearrange("(p t) j -> p t j", t=TPC)
                 if gb == NCH - 1:
                     nc.sync.dma_start(out=dst[:, 2 * qb:2 * qb + 2, :], in_=o_sb[:, 2 * qb:2 * qb + 2, :])
                 elif qb == PPC - 1:
                     nc.sync.dma_start(out=dst, in_=o_sb[:])
-            if (j - LAG_RED) % 2 == 0 and 0 <= (j - LAG_RED) // 2 < NPAIR // 2:
-                r = (j - LAG_RED) // 2
-                if r % 2 == 0:
-                    nc.scalar.mul(out=nx2[:, 4 * r:4 * r + 4], in_=x2h[:, 4 * r:4 * r + 4], mul=-1.0)
-            if (j - LAG_RED) % 2 == 0 and 0 <= (j - LAG_RED) // 2 < NPAIR // 2:
-                r = (j - LAG_RED) // 2
-                if r % 2 == 1:
-                    for slot in range(4):
+            for r in due:
+                n = min(4, 2 * len(B_PAIRS) - 4 * r)
+                if r % 3 != 1:
+                    nc.scalar.mul(out=nx2[:, 4 * r:4 * r + n], in_=x2h[:, 4 * r:4 * r + n], mul=-1.0)
+                else:
+                    for slot in range(n):
                         junk = jpool.tile([P, P], BF16, name="junk")
                         nc.scalar.activation(
                             out=junk[:], in_=accs[r][:, slot, :], func=ACT.Identity, scale=-1.0,

@@ -139,6 +139,11 @@ def tile_rbf_kernel_t_kernel(tc, X, Z, l_raw, sigma_f_raw, out):
 
         w4h = const.tile([P, 4], F32)
         nc.vector.tensor_scalar_mul(out=w4h[:], in0=w4[:], scalar1=math.sqrt(0.5))
+        rep = const.tile([P, 4, P], F32)
+        nc.scalar.copy(out=rep[:], in_=w4[:].unsqueeze(2).to_broadcast([P, 4, P]))
+        wbank = psc.tile([P, 4, P], F32, tag="cr", name="wbank")
+        for t in range(4):
+            nc.tensor.transpose(wbank[:, t, :], rep[:, t, :], ident[:])
         sqz = raw_squares(zbank)
         sqs = {0: squares(xbanks[0])}
         lnsig = const.tile([P, 1], F32)
@@ -150,11 +155,6 @@ def tile_rbf_kernel_t_kernel(tc, X, Z, l_raw, sigma_f_raw, out):
         )
         zgrp = const.tile([P, 2 * P, 4], BF16, align_bytes=64)
         scale_out(zbank, zgrp[:])
-        rep = const.tile([P, 4, P], F32)
-        nc.vector.tensor_copy(out=rep[:], in_=w4[:].unsqueeze(2).to_broadcast([P, 4, P]))
-        wbank = psc.tile([P, 4, P], F32, tag="cr", name="wbank")
-        for t in range(4):
-            nc.tensor.transpose(wbank[:, t, :], rep[:, t, :], ident[:])
         w_b = const.tile([P, D], F32)
         w_b2 = w_b[:].unsqueeze(1).to_broadcast([P, 2, D])
 
@@ -167,9 +167,6 @@ def tile_rbf_kernel_t_kernel(tc, X, Z, l_raw, sigma_f_raw, out):
 
         zc = const.tile([P, 2 * P], U32, align_bytes=64)
         zsc = const.tile([P, 2 * P], U8, align_bytes=64)
-        nc.vector.quantize_mx(
-            out=zc[:].bitcast(FP8X4), scales=zsc[:], in_=zgrp[:].rearrange("p c t -> p (c t)")
-        )
         nz2b = const.tile([P, M_COLS], F32)
         nz2b2 = nz2b[:].unsqueeze(1).to_broadcast([P, 2, M_COLS])
         x2h = const.tile([P, 4 * N_ACC], F32)
@@ -246,12 +243,15 @@ def tile_rbf_kernel_t_kernel(tc, X, Z, l_raw, sigma_f_raw, out):
             due = [r for r in range(N_ACC) if B_PAIRS[min(2 * r + 1, len(B_PAIRS) - 1)] + LAG_RED == j]
             for r in due:
                 n = min(4, 2 * len(B_PAIRS) - 4 * r)
-                if r % 3 != 1:
+                if r % 3 == 0:
                     nc.vector.tensor_reduce(
                         out=x2h[:, 4 * r:4 * r + n], in_=accs[r][:, 0:n, :], axis=mybir.AxisListType.X, op=ALU.add
                     )
             if j == 0:
-                nc.vector.tensor_copy(
+                nc.vector.quantize_mx(
+                    out=zc[:].bitcast(FP8X4), scales=zsc[:], in_=zgrp[:].rearrange("p c t -> p (c t)")
+                )
+                nc.scalar.copy(
                     out=w_b[:].rearrange("m (u p e) -> m u p e", u=2, e=2),
                     in_=wbank[:].rearrange("m (u e) p -> m u p e", u=2),
                 )
@@ -282,7 +282,7 @@ def tile_rbf_kernel_t_kernel(tc, X, Z, l_raw, sigma_f_raw, out):
                     nc.sync.dma_start(out=dst, in_=o_sb[:])
             for r in due:
                 n = min(4, 2 * len(B_PAIRS) - 4 * r)
-                if r % 3 != 1:
+                if r % 3 == 0:
                     nc.scalar.mul(out=nx2[:, 4 * r:4 * r + n], in_=x2h[:, 4 * r:4 * r + n], mul=-1.0)
                 else:
                     for slot in range(n):

@@ -17,286 +17,251 @@ N_ROWS = 8192
 M_COLS = 256
 D = 512
 LIM = 36.0
-TPC = 8
-PPC = TPC // 2
-CHUNK = P * TPC
-NCH = N_ROWS // CHUNK
-NPAIR = NCH * PPC
+NT = D // P
+TPG = 4
+GROUP = P * TPG
+NG = N_ROWS // GROUP
 FLOPS = 2 * N_ROWS * M_COLS * D
-
-XT_BANKS = 3
-LEAD_SQ = 1
-LAG_RED = 2
-G_PAIRS = tuple(range(5, NPAIR, PPC))
-B_PAIRS = tuple(j for j in range(NPAIR) if j not in G_PAIRS)
-N_ACC = (len(B_PAIRS) + 1) // 2
-LAG_E1 = 4
-LAG_E2 = 5
 
 
 def tile_rbf_kernel_t_kernel(tc, X, Z, l_raw, sigma_f_raw, out):
     nc = tc.nc
     with ExitStack() as ctx:
         const = ctx.enter_context(tc.tile_pool(name="const", bufs=1))
-        xpool = ctx.enter_context(tc.tile_pool(name="xpool", bufs=NCH))
+        xpool = ctx.enter_context(tc.tile_pool(name="xpool", bufs=NG))
+        ppool = ctx.enter_context(tc.tile_pool(name="ppool", bufs=2))
         gpool = ctx.enter_context(tc.tile_pool(name="gpool", bufs=2))
-        spool = ctx.enter_context(tc.tile_pool(name="spool", bufs=4))
-        tpool = ctx.enter_context(tc.tile_pool(name="tpool", bufs=6))
-        jpool = ctx.enter_context(tc.tile_pool(name="jpool", bufs=2))
-        ypool = ctx.enter_context(tc.tile_pool(name="ypool", bufs=1))
+        spool = ctx.enter_context(tc.tile_pool(name="spool", bufs=3))
+        tpool = ctx.enter_context(tc.tile_pool(name="tpool", bufs=3))
         opool = ctx.enter_context(tc.tile_pool(name="opool", bufs=3))
-        psx = ctx.enter_context(tc.psum_pool(name="psx", bufs=XT_BANKS))
-        psc = ctx.enter_context(tc.psum_pool(name="psc", bufs=3))
+        psx = ctx.enter_context(tc.psum_pool(name="psx", bufs=2))
+        psc = ctx.enter_context(tc.psum_pool(name="psc", bufs=2))
         psa = ctx.enter_context(tc.psum_pool(name="psa", bufs=2))
         ctx.enter_context(tc.manual_schedule())
 
-        small = const.tile([P, 32], BF16)
-        nc.vector.memset(small[:], 0.0)
-        with nc.allow_non_contiguous_dma(reason="l_raw, two features to a partition"):
-            nc.sync.dma_start(
-                out=small[:, 0:4].rearrange("p (u e) -> p u e", u=2),
-                in_=l_raw.rearrange("(u p e) -> p u e", u=2, e=2),
-            )
-            nc.scalar.dma_start(out=small[:, 16:17], in_=sigma_f_raw.partition_broadcast(P))
-        z_sb = const.tile([P, 2, D], BF16)
-        nc.sync.dma_start(out=z_sb[:], in_=Z.rearrange("(h p) k -> p h k", p=P))
+        lrow = const.tile([P, P], BF16)
+        nc.vector.memset(lrow[:], 0.0)
+        sig = const.tile([P, 16], BF16)
+        nc.sync.dma_start(out=lrow[0:NT, :], in_=l_raw.rearrange("(t k) -> t k", k=P))
+        with nc.allow_non_contiguous_dma(reason="one value to all partitions"):
+            nc.scalar.dma_start(out=sig[:, 0:1], in_=sigma_f_raw.partition_broadcast(P))
         xs = []
-        for c in range(NCH):
-            x_sb = xpool.tile([P, TPC, D], BF16, name="x_sb")
+
+        def load(g):
+            x_sb = xpool.tile([P, TPG, D], BF16, name="x_sb")
             nc.sync.dma_start(
                 out=x_sb[:],
-                in_=X[c * CHUNK:(c + 1) * CHUNK, :].rearrange("(p t) k -> p t k", t=TPC),
+                in_=X[g * GROUP:(g + 1) * GROUP, :].rearrange("(p t) k -> p t k", t=TPG),
             )
             xs.append(x_sb)
 
+        load(0)
+        z_sb = const.tile([P, 2, D], BF16)
+        nc.sync.dma_start(out=z_sb[:], in_=Z.rearrange("(h p) k -> p h k", p=P))
+        for g in range(1, NG):
+            load(g)
+
+        identb = const.tile([P, P], BF16)
+        make_identity(nc, identb[:])
         ident = const.tile([P, P], F32)
         make_identity(nc, ident[:])
 
-        def transposes(src_pair, bank):
-            for i, src in enumerate(src_pair):
-                words = src.bitcast(F32)
-                for u in range(2):
-                    nc.tensor.transpose(
-                        bank[:, u, i * P:(i + 1) * P], words[:, u * P:(u + 1) * P], ident[:]
-                    )
+        banks = {}
 
-        def pair_rows(j):
-            c, q = divmod(j, PPC)
-            return xs[c][:, 2 * q:2 * q + 2, :]
+        def stage_t(g):
+            pair = []
+            for h in range(2):
+                bank = psx.tile([P, 1024], BF16, tag="xb" + str(h), name="xbank")
+                pair.append(bank)
+            for h in range(2):
+                view = pair[h][:].rearrange("p (t c) -> p t c", t=2)
+                for tt in range(2):
+                    t = 2 * h + tt
+                    for i in range(TPG):
+                        nc.tensor.transpose(
+                            view[:, tt, i * P:(i + 1) * P], xs[g][:, i, t * P:(t + 1) * P], identb[:]
+                        )
+            banks[g] = pair
 
-        xbanks = {}
+        lbank = psa.tile([P, 1024], BF16, tag="acc", name="lbank")
+        nc.tensor.transpose(lbank[:, 0:P], lrow[:], identb[:])
+        stage_t(0)
+        zbank = psc.tile([P, NT, 2 * P], BF16, tag="cr", name="zbank")
+        for i in range(2):
+            for t in range(NT):
+                nc.tensor.transpose(zbank[:, t, i * P:(i + 1) * P], z_sb[:, i, t * P:(t + 1) * P], identb[:])
+        stage_t(1)
 
-        def stage_t(j):
-            bank = psx.tile([P, 2, 2 * P], F32, name="xbank")
-            rows = pair_rows(j)
-            transposes([rows[:, 0, :], rows[:, 1, :]], bank)
-            xbanks[j] = bank
-
-        def raw_squares(bank):
-            sq = spool.tile([P, 4, 2 * P], F32, name="sq")
-            nc.scalar.activation(
-                out=sq[:].rearrange("p (u e) c -> p u c e", u=2),
-                in_=bank[:].bitcast(BF16).rearrange("p u (c e) -> p u c e", e=2),
-                func=ACT.Square,
-            )
-            return sq
-
-        def squares(bank):
-            sq = spool.tile([P, 4, 2 * P], F32, name="sq")
-            halves = bank[:].bitcast(BF16).rearrange("p u (c e) -> p u c e", e=2)
-            for u in range(2):
-                for e in range(2):
-                    t = 2 * u + e
-                    nc.scalar.activation(
-                        out=sq[:, t, :], in_=halves[:, u, :, e], func=ACT.Square, scale=w4h[:, t:t + 1]
-                    )
-            return sq
-
-        zbank = psc.tile([P, 2, 2 * P], F32, tag="cr", name="zbank")
-        transposes([z_sb[:, 0, :], z_sb[:, 1, :]], zbank)
-        for j in range(XT_BANKS):
-            stage_t(j)
-
+        raw = const.tile([P, 32], F32)
         capped = const.tile([P, 32], F32)
-        nc.vector.tensor_scalar_min(out=capped[:], in0=small[:], scalar1=LIM)
         expv = const.tile([P, 32], F32)
-        nc.scalar.activation(out=expv[:], in_=capped[:], func=ACT.Exp)
         logv = const.tile([P, 32], F32)
-        nc.scalar.activation(out=logv[:], in_=expv[:], func=ACT.Ln, bias=1.0)
         splus = const.tile([P, 32], F32)
-        nc.vector.tensor_tensor(out=splus[:], in0=logv[:], in1=small[:], op=ALU.max)
-        w4 = const.tile([P, 4], F32)
-        nc.vector.reciprocal(out=w4[:], in_=splus[:, 0:4])
-        w4_b = w4[:].rearrange("p (o u e) -> p o u e", o=1, u=2).to_broadcast([P, 2 * P, 2, 2])
 
-        def scale_out(bank, grouped):
+        def softplus(cols):
+            nc.scalar.activation(out=expv[:, cols], in_=capped[:, cols], func=ACT.Exp)
+
+        def softplus_log(cols):
+            nc.scalar.activation(out=logv[:, cols], in_=expv[:, cols], func=ACT.Ln, bias=1.0)
+
+        lc = slice(0, NT)
+        sc = slice(16, 17)
+        nc.vector.tensor_scalar_min(out=capped[:, lc], in0=lbank[:, 0:NT], scalar1=LIM)
+        nc.vector.tensor_copy(out=raw[:, lc], in_=lbank[:, 0:NT])
+        nc.vector.tensor_scalar_min(out=capped[:, sc], in0=sig[:, 0:1], scalar1=LIM)
+        nc.vector.tensor_copy(out=raw[:, sc], in_=sig[:, 0:1])
+        softplus(lc)
+        softplus(sc)
+        softplus_log(lc)
+        softplus_log(sc)
+        nc.vector.tensor_tensor(out=splus[:, lc], in0=logv[:, lc], in1=raw[:, lc], op=ALU.max)
+        w4 = const.tile([P, NT], F32)
+        nc.vector.reciprocal(out=w4[:], in_=splus[:, lc])
+        w4h = const.tile([P, NT], F32)
+        nc.vector.tensor_scalar_mul(out=w4h[:], in0=w4[:], scalar1=math.sqrt(0.5))
+        nc.vector.tensor_tensor(out=splus[:, sc], in0=logv[:, sc], in1=raw[:, sc], op=ALU.max)
+        lnsig = const.tile([P, 1], F32)
+        nc.scalar.activation(out=lnsig[:], in_=splus[:, sc], func=ACT.Ln)
+        w4_b = w4[:].unsqueeze(1).to_broadcast([P, 2 * P, NT])
+
+        def scale_direct(bank, grouped):
             nc.vector.tensor_tensor(
-                out=grouped.rearrange("p c (u e) -> p c u e", u=2),
-                in0=bank[:].bitcast(BF16).rearrange("p u (c e) -> p c u e", e=2),
-                in1=w4_b,
-                op=ALU.mult,
+                out=grouped, in0=bank.rearrange("p (t c) -> p c t", t=NT), in1=w4_b, op=ALU.mult
             )
 
-        w4h = const.tile([P, 4], F32)
-        nc.vector.tensor_scalar_mul(out=w4h[:], in0=w4[:], scalar1=math.sqrt(0.5))
-        rep = const.tile([P, 4, P], F32)
-        nc.scalar.copy(out=rep[:], in_=w4[:].unsqueeze(2).to_broadcast([P, 4, P]))
-        wbank = psc.tile([P, 4, P], F32, tag="cr", name="wbank")
-        for t in range(4):
-            nc.tensor.transpose(wbank[:, t, :], rep[:, t, :], ident[:])
-        sqz = raw_squares(zbank)
-        sqs = {0: squares(xbanks[0])}
-        lnsig = const.tile([P, 1], F32)
-        nc.scalar.activation(out=lnsig[:], in_=splus[:, 16:17], func=ACT.Ln)
-
-        nw2 = const.tile([P, 4], F32)
+        nw2 = const.tile([P, NT], F32)
         nc.vector.scalar_tensor_tensor(
             out=nw2[:], in0=w4[:], scalar=-0.5, in1=w4[:], op0=ALU.mult, op1=ALU.mult
         )
-        zgrp = const.tile([P, 2 * P, 4], BF16, align_bytes=64)
-        scale_out(zbank, zgrp[:])
-        w_b = const.tile([P, D], F32)
-        w_b2 = w_b[:].unsqueeze(1).to_broadcast([P, 2, D])
 
+        sqz = const.tile([P, NT, 2 * P], F32)
+        nc.scalar.activation(out=sqz[:], in_=zbank[:], func=ACT.Square)
         z2bank = psc.tile([P, M_COLS], F32, tag="cr", name="z2bank")
-        for t in range(4):
+        for t in range(NT):
             nc.tensor.matmul(
                 out=z2bank[:], lhsT=nw2[:, t:t + 1].to_broadcast([P, P]), rhs=sqz[:, t, :],
-                start=(t == 0), stop=(t == 3),
+                start=(t == 0), stop=(t == NT - 1),
             )
 
+        zgrp = const.tile([P, 2 * P, NT], BF16, align_bytes=64)
         zc = const.tile([P, 2 * P], U32, align_bytes=64)
         zsc = const.tile([P, 2 * P], U8, align_bytes=64)
         nz2b = const.tile([P, M_COLS], F32)
-        nz2b2 = nz2b[:].unsqueeze(1).to_broadcast([P, 2, M_COLS])
-        x2h = const.tile([P, 4 * N_ACC], F32)
-        nx2 = const.tile([P, 4 * N_ACC], F32)
-        x2g = const.tile([P, 2 * len(G_PAIRS)], F32)
-        nx2g = const.tile([P, 2 * len(G_PAIRS)], F32)
+        x2h = const.tile([P, TPG * NG], F32)
 
-        def bias_of(pair, i):
-            if pair in G_PAIRS:
-                col = 2 * G_PAIRS.index(pair) + i
-                return nx2g[:, col:col + 1]
-            col = 2 * B_PAIRS.index(pair) + i
-            return nx2[:, col:col + 1]
-
-        def natural_norms(pair):
-            y32 = ypool.tile([P, 2, D], F32, name="y32")
-            nc.gpsimd.tensor_tensor(out=y32[:], in0=pair_rows(pair), in1=w_b2, op=ALU.mult)
-            col = 2 * G_PAIRS.index(pair)
-            for i in range(2):
-                junk = jpool.tile([P, D], BF16, tag="junkw", name="junkw")
-                nc.scalar.activation(
-                    out=junk[:], in_=y32[:, i, :], func=ACT.Square, scale=math.sqrt(0.5),
-                    accum_out=x2g[:, col + i:col + i + 1],
-                )
-            nc.scalar.mul(out=nx2g[:, col:col + 2], in_=x2g[:, col:col + 2], mul=-1.0)
-
+        planes = {}
         grps = {}
+        sqs = {}
+        accs = {}
         quant = {}
         crs = {}
         tmps = {}
-        outs = {}
-        accs = {}
 
-        def norms(pair):
-            r, half = divmod(B_PAIRS.index(pair), 2)
-            if half == 0:
-                accs[r] = psa.tile([P, 4, P], F32, name="acc")
-            for i in range(2):
-                for t in range(4):
-                    nc.tensor.matmul(
-                        out=accs[r][:, 2 * half + i, :], lhsT=sqs[pair][:, t, i * P:(i + 1) * P], rhs=ident[:],
-                        is_transpose=True, start=(t == 0), stop=(t == 3),
-                    )
-
-        def cross(pair):
-            gg, qq = divmod(pair, PPC)
-            xc, xsc = quant[gg]
-            cr = psc.tile([P, 2, M_COLS], F32, tag="cr", name="cr")
-            for i in range(2):
-                cols = slice((2 * qq + i) * P, (2 * qq + i + 1) * P)
-                nc.tensor.matmul_mx(
-                    out=cr[:, i, :],
-                    lhsT=xc[:, cols].bitcast(FP8X4), lhsT_scale=xsc[:, cols],
-                    rhs=zc[:].bitcast(FP8X4), rhs_scale=zsc[:],
-                    start=True, stop=True,
+        def scale(g):
+            planes[g] = ppool.tile([P, NT, GROUP], BF16, name="planes")
+            for t in range(NT):
+                nc.vector.tensor_scalar_mul(
+                    out=planes[g][:, t, :], in0=banks[g][t // 2][:, (t % 2) * GROUP:(t % 2 + 1) * GROUP],
+                    scalar1=w4[:, t:t + 1],
                 )
-            crs[pair] = cr
 
-        for j in range(NPAIR + LAG_E2 + 1):
-            g, q = divmod(j, PPC)
-            if j < NPAIR:
-                if j in B_PAIRS:
-                    norms(j)
-                if j + LEAD_SQ < NPAIR:
-                    if j + LEAD_SQ in G_PAIRS:
-                        natural_norms(j + LEAD_SQ)
-                    else:
-                        sqs[j + LEAD_SQ] = squares(xbanks[j + LEAD_SQ])
-                if q == 0:
-                    grps[g] = gpool.tile([P, TPC * P, 4], BF16, align_bytes=64, name="grp")
-                scale_out(xbanks[j], grps[g][:, q * 2 * P:(q + 1) * 2 * P, :])
-                if j + XT_BANKS < NPAIR:
-                    stage_t(j + XT_BANKS)
-            due = [r for r in range(N_ACC) if B_PAIRS[min(2 * r + 1, len(B_PAIRS) - 1)] + LAG_RED == j]
-            for r in due:
-                n = min(4, 2 * len(B_PAIRS) - 4 * r)
-                if r % 3 == 0:
-                    nc.vector.tensor_reduce(
-                        out=x2h[:, 4 * r:4 * r + n], in_=accs[r][:, 0:n, :], axis=mybir.AxisListType.X, op=ALU.add
+        def interleave(g):
+            grps[g] = gpool.tile([P, GROUP, NT], BF16, align_bytes=64, name="grp")
+            for i in range(TPG):
+                cols = slice(i * P, (i + 1) * P)
+                nc.gpsimd.tensor_scalar(
+                    out=grps[g][:, cols, :], in0=planes[g][:, :, cols].rearrange("p t c -> p c t"),
+                    scalar1=1.0, scalar2=0.0, op0=ALU.mult, op1=ALU.add,
+                )
+
+        def squares(g):
+            sq = spool.tile([P, NT, GROUP], F32, name="sq")
+            for t in range(NT):
+                nc.scalar.activation(
+                    out=sq[:, t, :], in_=banks[g][t // 2][:, (t % 2) * GROUP:(t % 2 + 1) * GROUP],
+                    func=ACT.Square, scale=w4h[:, t:t + 1],
+                )
+            sqs[g] = sq
+
+        def norms(g):
+            acc = psa.tile([P, TPG, P], F32, tag="acc", name="acc")
+            for i in range(TPG):
+                for t in range(NT):
+                    nc.tensor.matmul(
+                        out=acc[:, i, :], lhsT=sqs[g][:, t, i * P:(i + 1) * P], rhs=ident[:],
+                        is_transpose=True, start=(t == 0), stop=(t == NT - 1),
                     )
-            if j == 0:
+            accs[g] = acc
+
+        def reduce(g):
+            nc.vector.tensor_reduce(
+                out=x2h[:, TPG * g:TPG * (g + 1)], in_=accs[g][:], axis=mybir.AxisListType.X, op=ALU.add
+            )
+
+        def quantize(g):
+            xc = gpool.tile([P, GROUP], U32, align_bytes=64, name="xc")
+            xsc = gpool.tile([P, GROUP], U8, align_bytes=64, name="xsc")
+            nc.vector.quantize_mx(
+                out=xc[:].bitcast(FP8X4), scales=xsc[:], in_=grps[g][:].rearrange("p c t -> p (c t)")
+            )
+            quant[g] = (xc, xsc)
+
+        def cross(g):
+            xc, xsc = quant[g]
+            crs[g] = []
+            for q in range(2):
+                cr = psc.tile([P, 2, M_COLS], F32, tag="cr", name="cr")
+                for i in range(2):
+                    cols = slice((2 * q + i) * P, (2 * q + i + 1) * P)
+                    nc.tensor.matmul_mx(
+                        out=cr[:, i, :],
+                        lhsT=xc[:, cols].bitcast(FP8X4), lhsT_scale=xsc[:, cols],
+                        rhs=zc[:].bitcast(FP8X4), rhs_scale=zsc[:],
+                        start=True, stop=True,
+                    )
+                crs[g].append(cr)
+
+        def add(g):
+            tmp = tpool.tile([P, TPG, M_COLS], F32, name="tmp")
+            for i in range(TPG):
+                col = TPG * g + i
+                nc.vector.scalar_tensor_tensor(
+                    out=tmp[:, i, :], in0=crs[g][i // 2][:, i % 2, :], scalar=x2h[:, col:col + 1], in1=nz2b[:],
+                    op0=ALU.subtract, op1=ALU.add,
+                )
+            tmps[g] = tmp
+
+        def finish(g):
+            o_sb = opool.tile([P, TPG, M_COLS], F32, name="o_sb")
+            dst = out[g * GROUP:(g + 1) * GROUP, :].rearrange("(p t) j -> p t j", t=TPG)
+            parts = 2 if g == NG - 1 else 1
+            n = TPG // parts
+            for q in range(parts):
+                rows = slice(q * n, (q + 1) * n)
+                nc.scalar.activation(out=o_sb[:, rows, :], in_=tmps[g][:, rows, :], func=ACT.Exp)
+                nc.sync.dma_start(out=dst[:, rows, :], in_=o_sb[:, rows, :])
+
+        for s in range(NG + 2):
+            if 1 <= s < NG - 1:
+                stage_t(s + 1)
+            if s < NG:
+                scale(s)
+                interleave(s)
+                squares(s)
+            if s == 0:
+                scale_direct(zbank[:].rearrange("p t c -> p (t c)"), zgrp[:])
+            if s == 1:
                 nc.vector.quantize_mx(
                     out=zc[:].bitcast(FP8X4), scales=zsc[:], in_=zgrp[:].rearrange("p c t -> p (c t)")
                 )
-                nc.scalar.copy(
-                    out=w_b[:].rearrange("m (u p e) -> m u p e", u=2, e=2),
-                    in_=wbank[:].rearrange("m (u e) p -> m u p e", u=2),
-                )
-            if j == 1:
                 nc.vector.tensor_scalar_add(out=nz2b[:], in0=z2bank[:], scalar1=lnsig[:, 0:1])
-            a = j - LAG_E1
-            if 0 <= a < NPAIR:
-                tmp = tpool.tile([P, 2, M_COLS], F32, name="tmp")
-                nc.vector.tensor_tensor(out=tmp[:], in0=crs[a][:], in1=nz2b2, op=ALU.add)
-                tmps[a] = tmp
-                if a % PPC == 0:
-                    cross(a + PPC - 1)
-            b = j - LAG_E2
-            if 0 <= b < NPAIR:
-                gb, qb = divmod(b, PPC)
-                if qb == 0:
-                    outs[gb] = opool.tile([P, TPC, M_COLS], F32, name="o_sb")
-                o_sb = outs[gb]
-                for i in range(2):
-                    nc.scalar.activation(
-                        out=o_sb[:, 2 * qb + i, :], in_=tmps[b][:, i, :], func=ACT.Exp,
-                        bias=bias_of(b, i), scale=1.0,
-                    )
-                dst = out[gb * CHUNK:(gb + 1) * CHUNK, :].rearrange("(p t) j -> p t j", t=TPC)
-                if gb == NCH - 1:
-                    nc.sync.dma_start(out=dst[:, 2 * qb:2 * qb + 2, :], in_=o_sb[:, 2 * qb:2 * qb + 2, :])
-                elif qb == PPC - 1:
-                    nc.sync.dma_start(out=dst, in_=o_sb[:])
-            for r in due:
-                n = min(4, 2 * len(B_PAIRS) - 4 * r)
-                if r % 3 == 0:
-                    nc.scalar.mul(out=nx2[:, 4 * r:4 * r + n], in_=x2h[:, 4 * r:4 * r + n], mul=-1.0)
-                else:
-                    for slot in range(n):
-                        junk = jpool.tile([P, P], BF16, name="junk")
-                        nc.scalar.activation(
-                            out=junk[:], in_=accs[r][:, slot, :], func=ACT.Identity, scale=-1.0,
-                            accum_out=nx2[:, 4 * r + slot:4 * r + slot + 1],
-                        )
-            if j < NPAIR and q == PPC - 1:
-                xc = gpool.tile([P, TPC * P], U32, align_bytes=64, name="xc")
-                xsc = gpool.tile([P, TPC * P], U8, align_bytes=64, name="xsc")
-                nc.vector.quantize_mx(
-                    out=xc[:].bitcast(FP8X4), scales=xsc[:], in_=grps[g][:].rearrange("p c t -> p (c t)")
-                )
-                quant[g] = (xc, xsc)
-                for qq in range(PPC - 1):
-                    cross(g * PPC + qq)
+            if 1 <= s <= NG:
+                norms(s - 1)
+            if 2 <= s <= NG + 1:
+                add(s - 2)
+            if 1 <= s <= NG:
+                quantize(s - 1)
+                reduce(s - 1)
+                cross(s - 1)
+            if 2 <= s <= NG + 1:
+                finish(s - 2)

@@ -147,7 +147,8 @@ def tile_rbf_kernel_t_kernel(tc, X, Z, l_raw, sigma_f_raw, out):
         zc = const.tile([P, 2 * P], U32, align_bytes=64)
         zsc = const.tile([P, 2 * P], U8, align_bytes=64)
         nz2b = const.tile([P, M_COLS], F32)
-        x2h = const.tile([P, TPG * NG], F32)
+        nz2b2 = nz2b[:].unsqueeze(1).to_broadcast([P, 2, M_COLS])
+        nx2 = const.tile([P, TPG * NG], F32)
 
         planes = {}
         grps = {}
@@ -195,7 +196,8 @@ def tile_rbf_kernel_t_kernel(tc, X, Z, l_raw, sigma_f_raw, out):
 
         def reduce(g):
             nc.vector.tensor_reduce(
-                out=x2h[:, TPG * g:TPG * (g + 1)], in_=accs[g][:], axis=mybir.AxisListType.X, op=ALU.add
+                out=nx2[:, TPG * g:TPG * (g + 1)], in_=accs[g][:], axis=mybir.AxisListType.X, op=ALU.add,
+                negate=True,
             )
 
         def quantize(g):
@@ -223,11 +225,9 @@ def tile_rbf_kernel_t_kernel(tc, X, Z, l_raw, sigma_f_raw, out):
 
         def add(g):
             tmp = tpool.tile([P, TPG, M_COLS], F32, name="tmp")
-            for i in range(TPG):
-                col = TPG * g + i
-                nc.vector.scalar_tensor_tensor(
-                    out=tmp[:, i, :], in0=crs[g][i // 2][:, i % 2, :], scalar=x2h[:, col:col + 1], in1=nz2b[:],
-                    op0=ALU.subtract, op1=ALU.add,
+            for q in range(2):
+                nc.vector.tensor_tensor(
+                    out=tmp[:, 2 * q:2 * q + 2, :], in0=crs[g][q][:], in1=nz2b2, op=ALU.add
                 )
             tmps[g] = tmp
 
@@ -238,7 +238,11 @@ def tile_rbf_kernel_t_kernel(tc, X, Z, l_raw, sigma_f_raw, out):
             n = TPG // parts
             for q in range(parts):
                 rows = slice(q * n, (q + 1) * n)
-                nc.scalar.activation(out=o_sb[:, rows, :], in_=tmps[g][:, rows, :], func=ACT.Exp)
+                for i in range(q * n, (q + 1) * n):
+                    nc.scalar.activation(
+                        out=o_sb[:, i, :], in_=tmps[g][:, i, :], func=ACT.Exp,
+                        bias=nx2[:, TPG * g + i:TPG * g + i + 1],
+                    )
                 nc.sync.dma_start(out=dst[:, rows, :], in_=o_sb[:, rows, :])
 
         for s in range(NG + 2):

@@ -261,11 +261,14 @@ def tile_rbf_kernel_t_kernel(tc, X, Z, l_raw, sigma_f_raw, out):
                 nc.vector.tensor_scalar_add(out=nz2b[:], in0=z2bank[:], scalar1=lnsig[:, 0:1])
             if 1 <= s <= NG:
                 norms(s - 1)
-            if 2 <= s <= NG + 1:
-                add(s - 2)
-            if 1 <= s <= NG:
+            if 1 <= s < NG:
                 quantize(s - 1)
-                reduce(s - 1)
+                cross(s - 1)
+            if 2 <= s <= NG + 1:
+                reduce(s - 2)
+                add(s - 2)
+            if s == NG:
+                quantize(s - 1)
                 cross(s - 1)
             if 2 <= s <= NG + 1:
                 finish(s - 2)

@@ -30,6 +30,7 @@ def tile_rbf_kernel_t_kernel(tc, X, Z, l_raw, sigma_f_raw, out):
         const = ctx.enter_context(tc.tile_pool(name="const", bufs=1))
         xpool = ctx.enter_context(tc.tile_pool(name="xpool", bufs=NG))
         ppool = ctx.enter_context(tc.tile_pool(name="ppool", bufs=2))
+        grpool = ctx.enter_context(tc.tile_pool(name="grpool", bufs=1))
         gpool = ctx.enter_context(tc.tile_pool(name="gpool", bufs=2))
         spool = ctx.enter_context(tc.tile_pool(name="spool", bufs=3))
         tpool = ctx.enter_context(tc.tile_pool(name="tpool", bufs=3))
@@ -167,13 +168,11 @@ def tile_rbf_kernel_t_kernel(tc, X, Z, l_raw, sigma_f_raw, out):
                 )
 
         def interleave(g):
-            grps[g] = gpool.tile([P, GROUP, NT], BF16, align_bytes=64, name="grp")
-            for i in range(TPG):
-                cols = slice(i * P, (i + 1) * P)
-                nc.gpsimd.tensor_scalar(
-                    out=grps[g][:, cols, :], in0=planes[g][:, :, cols].rearrange("p t c -> p c t"),
-                    scalar1=1.0, scalar2=0.0, op0=ALU.mult, op1=ALU.add,
-                )
+            grps[g] = grpool.tile([P, GROUP, NT], BF16, align_bytes=64, name="grp")
+            nc.gpsimd.tensor_scalar(
+                out=grps[g][:], in0=planes[g][:].rearrange("p t c -> p c t"),
+                scalar1=1.0, scalar2=0.0, op0=ALU.mult, op1=ALU.add,
+            )
 
         def squares(g):
             sq = spool.tile([P, NT, GROUP], F32, name="sq")

@@ -18,6 +18,7 @@ M_COLS = 256
 D = 512
 LIM = 36.0
 NT = D // P
+PLAIN = 2
 TPG = 4
 GROUP = P * TPG
 NG = N_ROWS // GROUP
@@ -189,7 +190,7 @@ def tile_rbf_kernel_t_kernel(tc, X, Z, l_raw, sigma_f_raw, out):
                 for t in range(NT):
                     nc.tensor.matmul(
                         out=acc[:, i, :], lhsT=sqs[g][:, t, i * P:(i + 1) * P], rhs=ident[:],
-                        is_transpose=True, start=(t == 0), stop=(t == NT - 1),
+                        is_transpose=not (t == 0 and i < PLAIN), start=(t == 0), stop=(t == NT - 1),
                     )
             accs[g] = acc
 

@@ -17,7 +17,9 @@ N_ROWS = 8192
 M_COLS = 256
 D = 512
 LIM = 36.0
+LOG2E = 1.0 / math.log(2.0)
 NT = D // P
+WARM = 4
 PLAIN = 2
 TPG = 4
 GROUP = P * TPG
@@ -57,10 +59,9 @@ def tile_rbf_kernel_t_kernel(tc, X, Z, l_raw, sigma_f_raw, out):
             )
             xs.append(x_sb)
 
-        load(0)
         z_sb = const.tile([P, 2, D], BF16)
         nc.sync.dma_start(out=z_sb[:], in_=Z.rearrange("(h p) k -> p h k", p=P))
-        for g in range(1, NG):
+        for g in range(NG):
             load(g)
 
         identb = const.tile([P, P], BF16)
@@ -85,45 +86,49 @@ def tile_rbf_kernel_t_kernel(tc, X, Z, l_raw, sigma_f_raw, out):
                         )
             banks[g] = pair
 
+        warm = const.tile([P, P], F32)
+        nc.vector.memset(warm[:], 0.0)
+        wbank = psa.tile([P, TPG, P], F32, tag="acc", name="wbank")
+        for i in range(WARM):
+            nc.tensor.matmul(out=wbank[:, i, :], lhsT=warm[:], rhs=warm[:], start=True, stop=True)
         lbank = psa.tile([P, 1024], BF16, tag="acc", name="lbank")
         nc.tensor.transpose(lbank[:, 0:P], lrow[:], identb[:])
-        stage_t(0)
         zbank = psc.tile([P, NT, 2 * P], BF16, tag="cr", name="zbank")
         for i in range(2):
             for t in range(NT):
                 nc.tensor.transpose(zbank[:, t, i * P:(i + 1) * P], z_sb[:, i, t * P:(t + 1) * P], identb[:])
+        stage_t(0)
         stage_t(1)
 
         raw = const.tile([P, 32], F32)
-        capped = const.tile([P, 32], F32)
+        power = const.tile([P, 32], F32)
+        two = const.tile([P, 32], F32)
         expv = const.tile([P, 32], F32)
         logv = const.tile([P, 32], F32)
         splus = const.tile([P, 32], F32)
-
-        def softplus(cols):
-            nc.scalar.activation(out=expv[:, cols], in_=capped[:, cols], func=ACT.Exp)
-
-        def softplus_log(cols):
-            nc.scalar.activation(out=logv[:, cols], in_=expv[:, cols], func=ACT.Ln, bias=1.0)
-
+        nc.vector.memset(two[:], 2.0)
         lc = slice(0, NT)
         sc = slice(16, 17)
-        nc.vector.tensor_scalar_min(out=capped[:, lc], in0=lbank[:, 0:NT], scalar1=LIM)
-        nc.vector.tensor_copy(out=raw[:, lc], in_=lbank[:, 0:NT])
-        nc.vector.tensor_scalar_min(out=capped[:, sc], in0=sig[:, 0:1], scalar1=LIM)
-        nc.vector.tensor_copy(out=raw[:, sc], in_=sig[:, 0:1])
-        softplus(lc)
-        softplus(sc)
-        softplus_log(lc)
-        softplus_log(sc)
+
+        def exponential(cols, src):
+            nc.vector.tensor_scalar(
+                out=power[:, cols], in0=src, scalar1=LIM, scalar2=LOG2E, op0=ALU.min, op1=ALU.mult
+            )
+            nc.gpsimd.tensor_tensor(out=expv[:, cols], in0=two[:, cols], in1=power[:, cols], op=ALU.pow)
+            nc.vector.tensor_copy(out=raw[:, cols], in_=src)
+
+        exponential(lc, lbank[:, 0:NT])
+        exponential(sc, sig[:, 0:1])
+        nc.scalar.activation(out=logv[:, lc], in_=expv[:, lc], func=ACT.Ln, bias=1.0)
+        sqz = const.tile([P, NT, 2 * P], F32)
+        nc.scalar.activation(out=sqz[:], in_=zbank[:], func=ACT.Square)
+        nc.scalar.activation(out=logv[:, sc], in_=expv[:, sc], func=ACT.Ln, bias=1.0)
         nc.vector.tensor_tensor(out=splus[:, lc], in0=logv[:, lc], in1=raw[:, lc], op=ALU.max)
         w4 = const.tile([P, NT], F32)
         nc.vector.reciprocal(out=w4[:], in_=splus[:, lc])
+        lnsig = const.tile([P, 1], F32)
         w4h = const.tile([P, NT], F32)
         nc.vector.tensor_scalar_mul(out=w4h[:], in0=w4[:], scalar1=math.sqrt(0.5))
-        nc.vector.tensor_tensor(out=splus[:, sc], in0=logv[:, sc], in1=raw[:, sc], op=ALU.max)
-        lnsig = const.tile([P, 1], F32)
-        nc.scalar.activation(out=lnsig[:], in_=splus[:, sc], func=ACT.Ln)
         w4_b = w4[:].unsqueeze(1).to_broadcast([P, 2 * P, NT])
 
         def scale_direct(bank, grouped):
@@ -136,8 +141,6 @@ def tile_rbf_kernel_t_kernel(tc, X, Z, l_raw, sigma_f_raw, out):
             out=nw2[:], in0=w4[:], scalar=-0.5, in1=w4[:], op0=ALU.mult, op1=ALU.mult
         )
 
-        sqz = const.tile([P, NT, 2 * P], F32)
-        nc.scalar.activation(out=sqz[:], in_=zbank[:], func=ACT.Square)
         z2bank = psc.tile([P, M_COLS], F32, tag="cr", name="z2bank")
         for t in range(NT):
             nc.tensor.matmul(
@@ -149,7 +152,6 @@ def tile_rbf_kernel_t_kernel(tc, X, Z, l_raw, sigma_f_raw, out):
         zc = const.tile([P, 2 * P], U32, align_bytes=64)
         zsc = const.tile([P, 2 * P], U8, align_bytes=64)
         nz2b = const.tile([P, M_COLS], F32)
-        nz2b2 = nz2b[:].unsqueeze(1).to_broadcast([P, 2, M_COLS])
         nx2 = const.tile([P, TPG * NG], F32)
 
         planes = {}
@@ -225,9 +227,11 @@ def tile_rbf_kernel_t_kernel(tc, X, Z, l_raw, sigma_f_raw, out):
 
         def add(g):
             tmp = tpool.tile([P, TPG, M_COLS], F32, name="tmp")
-            for q in range(2):
-                nc.vector.tensor_tensor(
-                    out=tmp[:, 2 * q:2 * q + 2, :], in0=crs[g][q][:], in1=nz2b2, op=ALU.add
+            for i in range(TPG):
+                col = TPG * g + i
+                nc.vector.scalar_tensor_tensor(
+                    out=tmp[:, i, :], in0=crs[g][i // 2][:, i % 2, :], scalar=nx2[:, col:col + 1], in1=nz2b[:],
+                    op0=ALU.add, op1=ALU.add,
                 )
             tmps[g] = tmp
 
@@ -238,11 +242,7 @@ def tile_rbf_kernel_t_kernel(tc, X, Z, l_raw, sigma_f_raw, out):
             n = TPG // parts
             for q in range(parts):
                 rows = slice(q * n, (q + 1) * n)
-                for i in range(q * n, (q + 1) * n):
-                    nc.scalar.activation(
-                        out=o_sb[:, i, :], in_=tmps[g][:, i, :], func=ACT.Exp,
-                        bias=nx2[:, TPG * g + i:TPG * g + i + 1],
-                    )
+                nc.scalar.activation(out=o_sb[:, rows, :], in_=tmps[g][:, rows, :], func=ACT.Exp)
                 nc.sync.dma_start(out=dst[:, rows, :], in_=o_sb[:, rows, :])
 
         for s in range(NG + 2):
@@ -253,6 +253,8 @@ def tile_rbf_kernel_t_kernel(tc, X, Z, l_raw, sigma_f_raw, out):
                 interleave(s)
                 squares(s)
             if s == 0:
+                nc.vector.tensor_tensor(out=splus[:, sc], in0=logv[:, sc], in1=raw[:, sc], op=ALU.max)
+                nc.scalar.activation(out=lnsig[:], in_=splus[:, sc], func=ACT.Ln)
                 scale_direct(zbank[:].rearrange("p t c -> p (t c)"), zgrp[:])
             if s == 1:
                 nc.vector.quantize_mx(

@@ -238,7 +238,7 @@ def tile_rbf_kernel_t_kernel(tc, X, Z, l_raw, sigma_f_raw, out):
         def finish(g):
             o_sb = opool.tile([P, TPG, M_COLS], F32, name="o_sb")
             dst = out[g * GROUP:(g + 1) * GROUP, :].rearrange("(p t) j -> p t j", t=TPG)
-            parts = 2 if g == NG - 1 else 1
+            parts = TPG if g == NG - 1 else 1
             n = TPG // parts
             for q in range(parts):
                 rows = slice(q * n, (q + 1) * n)
@@ -263,11 +263,12 @@ def tile_rbf_kernel_t_kernel(tc, X, Z, l_raw, sigma_f_raw, out):
                 nc.vector.tensor_scalar_add(out=nz2b[:], in0=z2bank[:], scalar1=lnsig[:, 0:1])
             if 1 <= s <= NG:
                 norms(s - 1)
+            if 2 <= s <= NG + 1:
+                reduce(s - 2)
             if 1 <= s < NG:
                 quantize(s - 1)
                 cross(s - 1)
             if 2 <= s <= NG + 1:
-                reduce(s - 2)
                 add(s - 2)
             if s == NG:
                 quantize(s - 1)

import math
from contextlib import ExitStack

import concourse.mybir as mybir
from concourse.masks import make_identity

F32 = mybir.dt.float32
BF16 = mybir.dt.bfloat16
U32 = mybir.dt.uint32
U8 = mybir.dt.uint8
FP8X4 = mybir.dt.float8_e4m3fn_x4
ALU = mybir.AluOpType
ACT = mybir.ActivationFunctionType

P = 128
N_ROWS = 8192
M_COLS = 256
D = 512
LIM = 36.0
LOG2E = 1.0 / math.log(2.0)
NT = D // P
WARM = 4
PLAIN = 2
TPG = 4
GROUP = P * TPG
NG = N_ROWS // GROUP
FLOPS = 2 * N_ROWS * M_COLS * D


def tile_rbf_kernel_t_kernel(tc, X, Z, l_raw, sigma_f_raw, out):
    nc = tc.nc
    with ExitStack() as ctx:
        const = ctx.enter_context(tc.tile_pool(name="const", bufs=1))
        xpool = ctx.enter_context(tc.tile_pool(name="xpool", bufs=NG))
        ppool = ctx.enter_context(tc.tile_pool(name="ppool", bufs=2))
        grpool = ctx.enter_context(tc.tile_pool(name="grpool", bufs=1))
        gpool = ctx.enter_context(tc.tile_pool(name="gpool", bufs=2))
        spool = ctx.enter_context(tc.tile_pool(name="spool", bufs=3))
        tpool = ctx.enter_context(tc.tile_pool(name="tpool", bufs=3))
        opool = ctx.enter_context(tc.tile_pool(name="opool", bufs=3))
        psx = ctx.enter_context(tc.psum_pool(name="psx", bufs=2))
        psc = ctx.enter_context(tc.psum_pool(name="psc", bufs=2))
        psa = ctx.enter_context(tc.psum_pool(name="psa", bufs=2))
        ctx.enter_context(tc.manual_schedule())

        lrow = const.tile([P, P], BF16)
        nc.vector.memset(lrow[:], 0.0)
        sig = const.tile([P, 16], BF16)
        nc.sync.dma_start(out=lrow[0:NT, :], in_=l_raw.rearrange("(t k) -> t k", k=P))
        with nc.allow_non_contiguous_dma(reason="one value to all partitions"):
            nc.scalar.dma_start(out=sig[:, 0:1], in_=sigma_f_raw.partition_broadcast(P))
        xs = []

        def load(g):
            x_sb = xpool.tile([P, TPG, D], BF16, name="x_sb")
            nc.sync.dma_start(
                out=x_sb[:],
                in_=X[g * GROUP:(g + 1) * GROUP, :].rearrange("(p t) k -> p t k", t=TPG),
            )
            xs.append(x_sb)

        z_sb = const.tile([P, 2, D], BF16)
        nc.sync.dma_start(out=z_sb[:], in_=Z.rearrange("(h p) k -> p h k", p=P))
        for g in range(NG):
            load(g)

        identb = const.tile([P, P], BF16)
        make_identity(nc, identb[:])
        ident = const.tile([P, P], F32)
        make_identity(nc, ident[:])

        banks = {}

        def stage_t(g):
            pair = []
            for h in range(2):
                bank = psx.tile([P, 1024], BF16, tag="xb" + str(h), name="xbank")
                pair.append(bank)
            for h in range(2):
                view = pair[h][:].rearrange("p (t c) -> p t c", t=2)
                for tt in range(2):
                    t = 2 * h + tt
                    for i in range(TPG):
                        nc.tensor.transpose(
                            view[:, tt, i * P:(i + 1) * P], xs[g][:, i, t * P:(t + 1) * P], identb[:]
                        )
            banks[g] = pair

        warm = const.tile([P, P], F32)
        nc.vector.memset(warm[:], 0.0)
        wbank = psa.tile([P, TPG, P], F32, tag="acc", name="wbank")
        for i in range(WARM):
            nc.tensor.matmul(out=wbank[:, i, :], lhsT=warm[:], rhs=warm[:], start=True, stop=True)
        lbank = psa.tile([P, 1024], BF16, tag="acc", name="lbank")
        nc.tensor.transpose(lbank[:, 0:P], lrow[:], identb[:])
        zbank = psc.tile([P, NT, 2 * P], BF16, tag="cr", name="zbank")
        for i in range(2):
            for t in range(NT):
                nc.tensor.transpose(zbank[:, t, i * P:(i + 1) * P], z_sb[:, i, t * P:(t + 1) * P], identb[:])
        stage_t(0)
        stage_t(1)

        raw = const.tile([P, 32], F32)
        power = const.tile([P, 32], F32)
        two = const.tile([P, 32], F32)
        expv = const.tile([P, 32], F32)
        logv = const.tile([P, 32], F32)
        splus = const.tile([P, 32], F32)
        nc.vector.memset(two[:], 2.0)
        lc = slice(0, NT)
        sc = slice(16, 17)

        def exponential(cols, src):
            nc.vector.tensor_scalar(
                out=power[:, cols], in0=src, scalar1=LIM, scalar2=LOG2E, op0=ALU.min, op1=ALU.mult
            )
            nc.gpsimd.tensor_tensor(out=expv[:, cols], in0=two[:, cols], in1=power[:, cols], op=ALU.pow)
            nc.vector.tensor_copy(out=raw[:, cols], in_=src)

        exponential(lc, lbank[:, 0:NT])
        exponential(sc, sig[:, 0:1])
        nc.scalar.activation(out=logv[:, lc], in_=expv[:, lc], func=ACT.Ln, bias=1.0)
        sqz = const.tile([P, NT, 2 * P], F32)
        nc.scalar.activation(out=sqz[:], in_=zbank[:], func=ACT.Square)
        nc.scalar.activation(out=logv[:, sc], in_=expv[:, sc], func=ACT.Ln, bias=1.0)
        nc.vector.tensor_tensor(out=splus[:, lc], in0=logv[:, lc], in1=raw[:, lc], op=ALU.max)
        w4 = const.tile([P, NT], F32)
        nc.vector.reciprocal(out=w4[:], in_=splus[:, lc])
        lnsig = const.tile([P, 1], F32)
        w4h = const.tile([P, NT], F32)
        nc.vector.tensor_scalar_mul(out=w4h[:], in0=w4[:], scalar1=math.sqrt(0.5))
        w4_b = w4[:].unsqueeze(1).to_broadcast([P, 2 * P, NT])

        def scale_direct(bank, grouped):
            nc.vector.tensor_tensor(
                out=grouped, in0=bank.rearrange("p (t c) -> p c t", t=NT), in1=w4_b, op=ALU.mult
            )

        nw2 = const.tile([P, NT], F32)
        nc.vector.scalar_tensor_tensor(
            out=nw2[:], in0=w4[:], scalar=-0.5, in1=w4[:], op0=ALU.mult, op1=ALU.mult
        )

        z2bank = psc.tile([P, M_COLS], F32, tag="cr", name="z2bank")
        for t in range(NT):
            nc.tensor.matmul(
                out=z2bank[:], lhsT=nw2[:, t:t + 1].to_broadcast([P, P]), rhs=sqz[:, t, :],
                start=(t == 0), stop=(t == NT - 1),
            )

        zgrp = const.tile([P, 2 * P, NT], BF16, align_bytes=64)
        zc = const.tile([P, 2 * P], U32, align_bytes=64)
        zsc = const.tile([P, 2 * P], U8, align_bytes=64)
        nz2b = const.tile([P, M_COLS], F32)
        nx2 = const.tile([P, TPG * NG], F32)

        planes = {}
        grps = {}
        sqs = {}
        accs = {}
        quant = {}
        crs = {}
        tmps = {}

        def scale(g):
            planes[g] = ppool.tile([P, NT, GROUP], BF16, name="planes")
            for t in range(NT):
                nc.vector.tensor_scalar_mul(
                    out=planes[g][:, t, :], in0=banks[g][t // 2][:, (t % 2) * GROUP:(t % 2 + 1) * GROUP],
                    scalar1=w4[:, t:t + 1],
                )

        def interleave(g):
            grps[g] = grpool.tile([P, GROUP, NT], BF16, align_bytes=64, name="grp")
            nc.gpsimd.tensor_scalar(
                out=grps[g][:], in0=planes[g][:].rearrange("p t c -> p c t"),
                scalar1=1.0, scalar2=0.0, op0=ALU.mult, op1=ALU.add,
            )

        def squares(g):
            sq = spool.tile([P, NT, GROUP], F32, name="sq")
            for t in range(NT):
                nc.scalar.activation(
                    out=sq[:, t, :], in_=banks[g][t // 2][:, (t % 2) * GROUP:(t % 2 + 1) * GROUP],
                    func=ACT.Square, scale=w4h[:, t:t + 1],
                )
            sqs[g] = sq

        def norms(g):
            acc = psa.tile([P, TPG, P], F32, tag="acc", name="acc")
            for i in range(TPG):
                for t in range(NT):
                    nc.tensor.matmul(
                        out=acc[:, i, :], lhsT=sqs[g][:, t, i * P:(i + 1) * P], rhs=ident[:],
                        is_transpose=not (t == 0 and i < PLAIN), start=(t == 0), stop=(t == NT - 1),
                    )
            accs[g] = acc

        def reduce(g):
            nc.vector.tensor_reduce(
                out=nx2[:, TPG * g:TPG * (g + 1)], in_=accs[g][:], axis=mybir.AxisListType.X, op=ALU.add,
                negate=True,
            )

        def quantize(g):
            xc = gpool.tile([P, GROUP], U32, align_bytes=64, name="xc")
            xsc = gpool.tile([P, GROUP], U8, align_bytes=64, name="xsc")
            nc.vector.quantize_mx(
                out=xc[:].bitcast(FP8X4), scales=xsc[:], in_=grps[g][:].rearrange("p c t -> p (c t)")
            )
            quant[g] = (xc, xsc)

        def cross(g):
            xc, xsc = quant[g]
            crs[g] = []
            for q in range(2):
                cr = psc.tile([P, 2, M_COLS], F32, tag="cr", name="cr")
                for i in range(2):
                    cols = slice((2 * q + i) * P, (2 * q + i + 1) * P)
                    nc.tensor.matmul_mx(
                        out=cr[:, i, :],
                        lhsT=xc[:, cols].bitcast(FP8X4), lhsT_scale=xsc[:, cols],
                        rhs=zc[:].bitcast(FP8X4), rhs_scale=zsc[:],
                        start=True, stop=True,
                    )
                crs[g].append(cr)

        def add(g):
            tmp = tpool.tile([P, TPG, M_COLS], F32, name="tmp")
            for i in range(TPG):
                col = TPG * g + i
                nc.vector.scalar_tensor_tensor(
                    out=tmp[:, i, :], in0=crs[g][i // 2][:, i % 2, :], scalar=nx2[:, col:col + 1], in1=nz2b[:],
                    op0=ALU.add, op1=ALU.add,
                )
            tmps[g] = tmp

        def finish(g):
            o_sb = opool.tile([P, TPG, M_COLS], F32, name="o_sb")
            dst = out[g * GROUP:(g + 1) * GROUP, :].rearrange("(p t) j -> p t j", t=TPG)
            parts = TPG if g == NG - 1 else 1
            n = TPG // parts
            for q in range(parts):
                rows = slice(q * n, (q + 1) * n)
                nc.scalar.activation(out=o_sb[:, rows, :], in_=tmps[g][:, rows, :], func=ACT.Exp)
                nc.sync.dma_start(out=dst[:, rows, :], in_=o_sb[:, rows, :])

        for s in range(NG + 2):
            if 1 <= s < NG - 1:
                stage_t(s + 1)
            if s < NG:
                scale(s)
                interleave(s)
                squares(s)
            if s == 0:
                nc.vector.tensor_tensor(out=splus[:, sc], in0=logv[:, sc], in1=raw[:, sc], op=ALU.max)
                nc.scalar.activation(out=lnsig[:], in_=splus[:, sc], func=ACT.Ln)
                scale_direct(zbank[:].rearrange("p t c -> p (t c)"), zgrp[:])
            if s == 1:
                nc.vector.quantize_mx(
                    out=zc[:].bitcast(FP8X4), scales=zsc[:], in_=zgrp[:].rearrange("p c t -> p (c t)")
                )
                nc.vector.tensor_scalar_add(out=nz2b[:], in0=z2bank[:], scalar1=lnsig[:, 0:1])
            if 1 <= s <= NG:
                norms(s - 1)
            if 2 <= s <= NG + 1:
                reduce(s - 2)
            if 1 <= s < NG:
                quantize(s - 1)
                cross(s - 1)
            if 2 <= s <= NG + 1:
                add(s - 2)
            if s == NG:
                quantize(s - 1)
                cross(s - 1)
            if 2 <= s <= NG + 1:
                finish(s - 2)
